import numpy as np
import ml_dtypes


def mxq(x, axis, fmt="e4m3"):
    dtype, down = {"e4m3": (ml_dtypes.float8_e4m3fn, 7), "e5m2": (ml_dtypes.float8_e5m2, 14)}[fmt]
    v = np.moveaxis(np.asarray(x, np.float32).astype(ml_dtypes.bfloat16).astype(np.float64), axis, -1)
    blocks = v.reshape(v.shape[:-1] + (-1, 32))
    amax = np.abs(blocks).max(-1, keepdims=True)
    byte = np.maximum(np.where(amax > 0, np.frexp(amax)[1] - 1 + 127, 0) - down, 1)
    scale = np.exp2(byte - 127.0)
    codes = (blocks / scale).astype(np.float32).astype(dtype).astype(np.float64)
    return np.moveaxis((codes * scale).reshape(v.shape), -1, axis)


WIDE = False


def mx_kscale(k):
    if not WIDE:
        return np.ones(k)
    levels = np.array([10, -10, 5, -5, 0])
    a = np.random.permutation(np.resize(levels, k // 512 * 4)).reshape(k // 512, 4)
    idx = np.arange(k)
    return np.exp2(a[idx // 512, idx % 128 // 32])


BF16 = ml_dtypes.bfloat16


def bf(x):
    return np.asarray(x, np.float32).astype(BF16)


def f64(x):
    return np.asarray(x).astype(np.float64)


B, D, DC, NREF = 8192, 512, 512, 256
KAPPA = 1.25


def logsumexp_rows(v):
    m = v.max(axis=1, keepdims=True)
    return np.log(np.exp(v - m).sum(axis=1)) + m[:, 0]


def setup_inputs():
    s = mx_kscale(D)
    h0 = np.exp(-2.0 * KAPPA / np.sqrt(DC)) / np.sqrt(2.0 * np.pi)
    sig = h0 * np.sqrt(2.0 * KAPPA) / DC ** 0.25
    return {"x": bf(np.random.standard_normal((B, D)) * s),
            "pca_weight": bf(np.random.standard_normal((DC, D)) * 0.95 * sig / np.sqrt(D) / s[None, :]),
            "pca_bias": bf(np.random.standard_normal(DC) * 0.3 * sig),
            "X_ref": bf(np.random.standard_normal((NREF, DC)) * sig),
            "bandwidth": bf(h0 * np.exp(np.random.standard_normal(1) * 2.0 / DC))}


def reference(x, pca_weight, pca_bias, X_ref, bandwidth):
    r = f64(X_ref)
    h = f64(bandwidth)
    z = (mxq(f64(x), 1, "e4m3") @ mxq(f64(pca_weight), 1, "e4m3").T) + f64(pca_bias)
    n, d = r.shape
    d2 = (np.sum(z * z, axis=-1, keepdims=True)
          + np.sum(r * r, axis=-1)[None, :]
          - 2.0 * (mxq(z, 1, "e4m3") @ mxq(r, 1, "e4m3").T))
    d2 = np.maximum(d2, 0.0)
    coeff = -np.log(n) - np.log(2.0 * np.pi) * d / 2.0 - np.log(h) * d
    logits = d2 / (-2.0 * h * h)
    return logsumexp_rows(logits) + coeff

@@ -1,0 +1,322 @@
+import math
+from contextlib import ExitStack
+
+import concourse.mybir as mybir
+from concourse.masks import make_identity
+
+FLOPS = 2 * 8192 * 512 * 512 + 2 * 8192 * 512 * 256
+
+F32 = mybir.dt.float32
+BF16 = mybir.dt.bfloat16
+U32 = mybir.dt.uint32
+U8 = mybir.dt.uint8
+I32 = mybir.dt.int32
+FP8X4 = mybir.dt.float8_e4m3fn_x4
+ALU = mybir.AluOpType
+ACT = mybir.ActivationFunctionType
+
+P = 128
+B = 8192
+D = 512
+DC = 512
+NREF = 256
+NT = B // P
+NPAIR = NT // 2
+CHUNKS = (2, 2, 4, 8, 8, 8, 8, 8, 8, 8)
+NZ2 = 32
+PS_BUFS = {"xT": 2, "Z": 4, "G": 1, "z2": 1}
+
+
+def tile_kernelloglikelihood_t_kernel(tc, x, pca_weight, pca_bias, X_ref, bandwidth, out):
+    nc = tc.nc
+    with ExitStack() as ctx:
+        ctx.enter_context(tc.manual_schedule())
+        const = ctx.enter_context(tc.tile_pool(name="const", bufs=1))
+        work = ctx.enter_context(tc.tile_pool(name="work", bufs=3))
+        psum = ctx.enter_context(tc.psum_pool(name="psum", bufs=2))
+
+        hb = const.tile([P, 1], BF16)
+        nc.scalar.dma_start(out=hb[:], in_=bandwidth.partition_broadcast(P))
+        bsb = const.tile([P, 4], BF16)
+        nc.scalar.dma_start(out=bsb[:], in_=pca_bias.rearrange("(p t) -> p t", t=4))
+        wsb = const.tile([P, 4, D], BF16)
+        nc.sync.dma_start(out=wsb[:], in_=pca_weight.rearrange("(p t) k -> p t k", t=4))
+        xv = x.rearrange("(p n) k -> p n k", n=NT)
+        xw = []
+        n0 = 0
+        rsb = const.tile([P, 2, DC], BF16)
+        for ci, cn in enumerate(CHUNKS):
+            xt = const.tile([P, cn, D], BF16, name="xchunk%d" % ci)
+            nc.sync.dma_start(out=xt[:], in_=xv[:, n0:n0 + cn, :])
+            xt32 = xt[:].bitcast(F32)
+            for k in range(cn):
+                xw.append(xt32[:, k, :])
+            n0 += cn
+            if ci == 0:
+                nc.sync.dma_start(out=rsb[:], in_=X_ref.rearrange("(p j) c -> p j c", j=2))
+
+        identf = const.tile([P, P], F32)
+        make_identity(nc, identf[:])
+
+        def small(name, dt=F32, w=1):
+            return const.tile([P, w], dt, name=name)
+
+        tps = {}
+        groupeds = {}
+
+        def transposes(key, srcs, tag):
+            tp = psum.tile([P, 2, 2, P], F32, tag=tag, bufs=PS_BUFS[tag], name="tp")
+            for a in range(2):
+                for u in range(2):
+                    nc.tensor.transpose(tp[:, a, u, :], srcs[2 * a + u], identf[:])
+            tps[key] = tp
+
+        def copy_out(key):
+            tp = tps.pop(key)
+            grouped = work.tile([P, 2 * P * 4], BF16, tag="grouped", bufs=3, align_bytes=64, name="grouped")
+            nc.scalar.copy(out=grouped[:].bitcast(F32).rearrange("p (a i u) -> p a i u", a=2, u=2),
+                           in_=tp[:].rearrange("p a u i -> p a i u"))
+            groupeds[key] = grouped
+
+        def quantise(key, codes, scales):
+            grouped = groupeds.pop(key)
+            nc.vector.quantize_mx(out=codes.bitcast(FP8X4), scales=scales, in_=grouped[:])
+
+        wc = const.tile([P, 4 * P], U32, align_bytes=64)
+        wsc = const.tile([P, 4 * P], U8, align_bytes=64)
+        w32 = wsb[:].bitcast(F32)
+        for a in range(2):
+            transposes("w%d" % a, [w32[:, 2 * a + (i // 2), P * (i % 2):P * (i % 2) + P] for i in range(4)], "xT")
+        for a in range(2):
+            copy_out("w%d" % a)
+        for a in range(2):
+            quantise("w%d" % a, wc[:, 256 * a:256 * a + 256], wsc[:, 256 * a:256 * a + 256])
+
+        h32 = small("h32")
+        nc.vector.tensor_copy(out=h32[:], in_=hb[:])
+        hh = small("hh")
+        nc.vector.tensor_tensor(out=hh[:], in0=h32[:], in1=h32[:], op=ALU.mult)
+        rh = small("rh")
+        nc.vector.reciprocal(out=rh[:], in_=hh[:])
+        n2s = small("n2s")
+        nc.vector.tensor_scalar(out=n2s[:], in0=rh[:], scalar1=-1.0, scalar2=None, op0=ALU.mult)
+        s_ap = small("s_ap")
+        nc.vector.tensor_scalar(out=s_ap[:], in0=rh[:], scalar1=0.5, scalar2=None, op0=ALU.mult)
+        negs = small("negs", w=NZ2)
+        nc.vector.tensor_scalar(out=negs[:], in0=rh[:, 0:1].to_broadcast([P, NZ2]), scalar1=-0.5,
+                                scalar2=None, op0=ALU.mult)
+        b32 = small("b32", w=4)
+        nc.vector.tensor_copy(out=b32[:], in_=bsb[:])
+
+        ei = small("ei", I32)
+        mi = small("mi", I32)
+        ef = small("ef")
+        gt = small("gt")
+        halve = small("halve")
+        m2 = small("m2")
+        e3 = small("e3")
+        den = small("den")
+        rden = small("rden")
+        wq = small("wq")
+        mant = mi[:].bitcast(F32)
+        ln_steps = [
+            lambda: nc.vector.tensor_single_scalar(out=ei[:], in_=h32[:].bitcast(I32), scalar=23,
+                                                   op=ALU.logical_shift_right),
+            lambda: nc.vector.tensor_scalar(out=mi[:], in0=h32[:].bitcast(I32), scalar1=0x007FFFFF,
+                                            scalar2=0x3F800000, op0=ALU.bitwise_and, op1=ALU.bitwise_or),
+            lambda: nc.vector.tensor_copy(out=ef[:], in_=ei[:]),
+            lambda: nc.vector.tensor_single_scalar(out=gt[:], in_=mant, scalar=math.sqrt(2.0), op=ALU.is_gt),
+            lambda: nc.vector.tensor_scalar(out=halve[:], in0=gt[:], scalar1=-0.5, scalar2=1.0,
+                                            op0=ALU.mult, op1=ALU.add),
+            lambda: nc.vector.tensor_tensor(out=m2[:], in0=mant, in1=halve[:], op=ALU.mult),
+            lambda: nc.vector.scalar_tensor_tensor(out=e3[:], in0=ef[:], scalar=-127.0, in1=gt[:],
+                                                   op0=ALU.add, op1=ALU.add),
+            lambda: nc.vector.tensor_scalar(out=den[:], in0=m2[:], scalar1=1.0, scalar2=None, op0=ALU.add),
+            lambda: nc.vector.reciprocal(out=rden[:], in_=den[:]),
+            lambda: nc.vector.scalar_tensor_tensor(out=wq[:], in0=m2[:], scalar=-1.0, in1=rden[:],
+                                                   op0=ALU.add, op1=ALU.mult),
+        ]
+        coeff = small("coeff")
+
+        def ln_series():
+            w2 = small("w2")
+            nc.gpsimd.tensor_tensor(out=w2[:], in0=wq[:], in1=wq[:], op=ALU.mult)
+            poly = small("poly0")
+            nc.gpsimd.tensor_scalar(out=poly[:], in0=w2[:], scalar1=1.0 / 17.0, scalar2=1.0 / 15.0,
+                                    op0=ALU.mult, op1=ALU.add)
+            for odd in (13, 11, 9, 7, 5, 3, 1):
+                nxt = small("poly%d" % odd)
+                nc.gpsimd.tensor_scalar(out=nxt[:], in0=poly[:], scalar1=w2[:, 0:1], scalar2=1.0 / odd,
+                                        op0=ALU.mult, op1=ALU.add)
+                poly = nxt
+            wp = small("wp")
+            nc.gpsimd.tensor_tensor(out=wp[:], in0=poly[:], in1=wq[:], op=ALU.mult)
+            c1 = small("c1")
+            nc.gpsimd.tensor_scalar(out=c1[:], in0=e3[:], scalar1=-DC * math.log(2.0),
+                                    scalar2=-math.log(NREF) - 0.5 * DC * math.log(2.0 * math.pi),
+                                    op0=ALU.mult, op1=ALU.add)
+            nc.gpsimd.tensor_scalar(out=coeff[:], in0=wp[:], scalar1=-2.0 * DC, scalar2=c1[:, 0:1],
+                                    op0=ALU.mult, op1=ALU.add)
+
+        rc = const.tile([P, NREF], U32, align_bytes=64)
+        rsc = const.tile([P, NREF], U8, align_bytes=64)
+        r32 = rsb[:].bitcast(F32)
+        r2 = small("r2", w=2)
+        rep = const.tile([P, 2, P], F32)
+        csb = const.tile([P, NREF], F32)
+
+        def r_squares():
+            for jt in range(2):
+                rjunk = work.tile([P, DC], BF16, tag="rjunk", bufs=2, name="rjunk")
+                nc.scalar.activation(out=rjunk[:], in_=rsb[:, jt, :], func=ACT.Square, accum_out=r2[:, jt:jt + 1])
+                nc.gpsimd.tensor_copy(out=rep[:, jt, :], in_=r2[:, jt:jt + 1].to_broadcast([P, P]))
+
+        mn_all = const.tile([P, NT], F32)
+        sum_all = const.tile([P, NT], F32)
+        nega_all = const.tile([P, NT], F32)
+
+        xcodes = {}
+        zps = {}
+        zgs = {}
+        qts = {}
+        zcodes = {}
+        z2ps = {}
+        gps = {}
+        us = {}
+        ucls = {}
+
+        def valid(k):
+            return 0 <= k < NPAIR
+
+        def t_x(k):
+            transposes(k, [xw[2 * k + (i // 2)][:, P * (i % 2):P * (i % 2) + P] for i in range(4)], "xT")
+
+        def q_x(k):
+            xc = work.tile([P, 2 * P], U32, tag="xc", bufs=3, align_bytes=64, name="xc")
+            xs = work.tile([P, 2 * P], U8, tag="xs", bufs=3, align_bytes=64, name="xs")
+            quantise(k, xc[:], xs[:])
+            xcodes[k] = (xc, xs)
+
+        def s1(k):
+            xc, xs = xcodes.pop(k)
+            for a in range(2):
+                zp = psum.tile([P, 4, P], F32, tag="Z", bufs=PS_BUFS["Z"], name="zp")
+                for t in range(4):
+                    nc.tensor.matmul_mx(out=zp[:, t, :],
+                                        lhsT=wc[:, P * t:P * t + P].bitcast(FP8X4), lhsT_scale=wsc[:, P * t:P * t + P],
+                                        rhs=xc[:, P * a:P * a + P].bitcast(FP8X4), rhs_scale=xs[:, P * a:P * a + P],
+                                        start=True, stop=True)
+                zps[(k, a)] = zp
+
+        def ev(k, a):
+            if a == 0:
+                zgs[k] = work.tile([P, 2, P, 4], BF16, tag="zg", bufs=2, align_bytes=64, name="zg")
+            nc.vector.tensor_tensor(out=zgs[k][:, a, :, :], in0=zps[(k, a)][:].rearrange("p t i -> p i t"),
+                                    in1=b32[:].unsqueeze(1).to_broadcast([P, P, 4]), op=ALU.add)
+
+        def sq(k, a):
+            zp = zps.pop((k, a))
+            q = work.tile([P, 4, P], F32, tag="q", bufs=4, name="q")
+            for t in range(4):
+                nc.scalar.activation(out=q[:, t, :], in_=zp[:, t, :], func=ACT.Square, bias=b32[:, t:t + 1], scale=1.0)
+            qts[(k, a)] = q
+
+        def q_z(k):
+            zg = zgs.pop(k)
+            zc = work.tile([P, 2 * P], U32, tag="zc", bufs=3, align_bytes=64, name="zc")
+            zs = work.tile([P, 2 * P], U8, tag="zs", bufs=3, align_bytes=64, name="zs")
+            nc.vector.quantize_mx(out=zc[:].bitcast(FP8X4), scales=zs[:], in_=zg[:].rearrange("p a i t -> p (a i t)"))
+            zcodes[k] = (zc, zs)
+
+        def s2(k):
+            zc, zs = zcodes.pop(k)
+            gp = psum.tile([P, 2, NREF], F32, tag="G", bufs=PS_BUFS["G"], name="gp")
+            for a in range(2):
+                nc.tensor.matmul_mx(out=gp[:, a, :],
+                                    lhsT=zc[:, P * a:P * a + P].bitcast(FP8X4), lhsT_scale=zs[:, P * a:P * a + P],
+                                    rhs=rc[:].bitcast(FP8X4), rhs_scale=rsc[:], start=True, stop=True)
+            gps[k] = gp
+
+        def z2(k):
+            z2p = psum.tile([P, 2, NZ2], F32, tag="z2", bufs=PS_BUFS["z2"], name="z2p")
+            for a in range(2):
+                q = qts.pop((k, a))
+                for t in range(4):
+                    nc.tensor.matmul(out=z2p[:, a, :], lhsT=q[:, t, :], rhs=negs[:], start=(t == 0), stop=(t == 3))
+            z2ps[k] = z2p
+
+        def nega(k):
+            nc.scalar.copy(out=nega_all[:, 2 * k:2 * k + 2], in_=z2ps.pop(k)[:, :, 0])
+
+        def stt(k):
+            u = work.tile([P, 2, NREF], F32, tag="u", bufs=2, name="u")
+            nc.vector.scalar_tensor_tensor(out=u[:], in0=gps.pop(k)[:], scalar=n2s[:, 0:1],
+                                           in1=csb[:].unsqueeze(1).to_broadcast([P, 2, NREF]),
+                                           op0=ALU.mult, op1=ALU.add)
+            us[k] = u
+
+        def cm(k, a):
+            if a == 0:
+                ucls[k] = work.tile([P, 2, NREF], F32, tag="ucl", bufs=2, name="ucl")
+            n = 2 * k + a
+            nc.vector.tensor_scalar(out=ucls[k][:, a, :], in0=us[k][:, a, :], scalar1=nega_all[:, n:n + 1], scalar2=None,
+                                    op0=ALU.max, op1=ALU.min, accum_out=mn_all[:, n:n + 1])
+
+        def ex(k, a):
+            n = 2 * k + a
+            ejunk = work.tile([P, NREF], BF16, tag="ejunk", bufs=2, name="ejunk")
+            nc.scalar.activation(out=ejunk[:], in_=ucls[k][:, a, :], func=ACT.Exp, bias=mn_all[:, n:n + 1], scale=-1.0,
+                                 accum_out=sum_all[:, n:n + 1])
+
+        for j in range(-3, NPAIR + 2):
+            if valid(j + 1):
+                s1(j + 1)
+            if valid(j - 1):
+                s2(j - 1)
+                z2(j - 1)
+            if valid(j + 3):
+                t_x(j + 3)
+            if j == -2:
+                transposes("r", [r32[:, i // 2, (i % 2):256:2] for i in range(4)], "Z")
+            if j == 0:
+                r2t = psum.tile([P, 2, P], F32, tag="G", bufs=PS_BUFS["G"], name="r2t")
+                for jt in range(2):
+                    nc.tensor.transpose(r2t[:, jt, :], rep[:, jt, :], identf[:])
+            if valid(j + 2):
+                copy_out(j + 2)
+            if j == -2:
+                copy_out("r")
+                r_squares()
+            for a in range(2):
+                if valid(j):
+                    ev(j, a)
+                    sq(j, a)
+                if valid(j - 2):
+                    cm(j - 2, a)
+                    ex(j - 2, a)
+            if valid(j + 2):
+                q_x(j + 2)
+            if j == -2:
+                quantise("r", rc[:], rsc[:])
+            if valid(j - 1):
+                stt(j - 1)
+            if valid(j):
+                q_z(j)
+            if valid(j - 1):
+                nega(j - 1)
+            if j == 0:
+                nc.scalar.activation(out=csb[:], in_=r2t[:].rearrange("p a j -> p (a j)"), func=ACT.Copy,
+                                     scale=s_ap[:, 0:1])
+            if 3 <= j < 3 + len(ln_steps):
+                ln_steps[j - 3]()
+            if j == 3 + len(ln_steps):
+                ln_series()
+
+        lns = const.tile([P, NT], F32)
+        nc.scalar.activation(out=lns[:], in_=sum_all[:], func=ACT.Ln)
+        t1 = const.tile([P, NT], F32)
+        nc.vector.tensor_tensor(out=t1[:], in0=lns[:], in1=mn_all[:], op=ALU.subtract)
+        res = const.tile([P, NT], F32)
+        nc.vector.scalar_tensor_tensor(out=res[:], in0=t1[:], scalar=coeff[:, 0:1], in1=nega_all[:],
+                                       op0=ALU.add, op1=ALU.add)
+        nc.sync.dma_start(out=out.rearrange("(p n) -> p n", n=NT), in_=res[:])

@@ -23,7 +23,7 @@ NREF = 256
 NT = B // P
 NPAIR = NT // 2
 CHUNKS = (2, 2, 4, 8, 8, 8, 8, 8, 8, 8)
-NZ2 = 32
+NZ2 = 2
 PS_BUFS = {"xT": 2, "Z": 4, "G": 1, "z2": 1}
 
 

@@ -23,7 +23,6 @@ NREF = 256
 NT = B // P
 NPAIR = NT // 2
 CHUNKS = (2, 2, 4, 8, 8, 8, 8, 8, 8, 8)
-NZ2 = 2
 PS_BUFS = {"xT": 2, "Z": 4, "G": 1, "z2": 1}
 
 
@@ -102,11 +101,14 @@ def tile_kernelloglikelihood_t_kernel(tc, x, pca_weight, pca_bias, X_ref, bandwi
         nc.vector.tensor_scalar(out=n2s[:], in0=rh[:], scalar1=-1.0, scalar2=None, op0=ALU.mult)
         s_ap = small("s_ap")
         nc.vector.tensor_scalar(out=s_ap[:], in0=rh[:], scalar1=0.5, scalar2=None, op0=ALU.mult)
-        negs = small("negs", w=NZ2)
-        nc.vector.tensor_scalar(out=negs[:], in0=rh[:, 0:1].to_broadcast([P, NZ2]), scalar1=-0.5,
-                                scalar2=None, op0=ALU.mult)
         b32 = small("b32", w=4)
         nc.vector.tensor_copy(out=b32[:], in_=bsb[:])
+        rinv = small("rinv")
+        nc.vector.reciprocal(out=rinv[:], in_=h32[:])
+        rsq = small("rsq")
+        nc.vector.tensor_scalar(out=rsq[:], in0=rinv[:], scalar1=math.sqrt(0.5), scalar2=None, op0=ALU.mult)
+        bsc = small("bsc", w=4)
+        nc.vector.tensor_scalar(out=bsc[:], in0=b32[:], scalar1=rsq[:, 0:1], scalar2=None, op0=ALU.mult)
 
         ei = small("ei", I32)
         mi = small("mi", I32)
@@ -173,7 +175,14 @@ def tile_kernelloglikelihood_t_kernel(tc, x, pca_weight, pca_bias, X_ref, bandwi
 
         mn_all = const.tile([P, NT], F32)
         sum_all = const.tile([P, NT], F32)
-        nega_all = const.tile([P, NT], F32)
+        nega_v = const.tile([P, NT], F32)
+        nega_s = const.tile([P, NT], F32)
+
+        def on_vector(k):
+            return k % 2 == 0
+
+        def nega_of(k):
+            return nega_v if on_vector(k) else nega_s
 
         xcodes = {}
         zps = {}
@@ -218,7 +227,8 @@ def tile_kernelloglikelihood_t_kernel(tc, x, pca_weight, pca_bias, X_ref, bandwi
             zp = zps.pop((k, a))
             q = work.tile([P, 4, P], F32, tag="q", bufs=4, name="q")
             for t in range(4):
-                nc.scalar.activation(out=q[:, t, :], in_=zp[:, t, :], func=ACT.Square, bias=b32[:, t:t + 1], scale=1.0)
+                nc.scalar.activation(out=q[:, t, :], in_=zp[:, t, :], func=ACT.Square, bias=bsc[:, t:t + 1],
+                                     scale=rsq[:, 0:1])
             qts[(k, a)] = q
 
         def q_z(k):
@@ -238,15 +248,25 @@ def tile_kernelloglikelihood_t_kernel(tc, x, pca_weight, pca_bias, X_ref, bandwi
             gps[k] = gp
 
         def z2(k):
-            z2p = psum.tile([P, 2, NZ2], F32, tag="z2", bufs=PS_BUFS["z2"], name="z2p")
+            z2p = psum.tile([P, 2, P], F32, tag="z2", bufs=PS_BUFS["z2"], name="z2p")
             for a in range(2):
                 q = qts.pop((k, a))
                 for t in range(4):
-                    nc.tensor.matmul(out=z2p[:, a, :], lhsT=q[:, t, :], rhs=negs[:], start=(t == 0), stop=(t == 3))
+                    nc.tensor.matmul(out=z2p[:, a, :], lhsT=q[:, t, :], rhs=identf[:], is_transpose=True,
+                                     start=(t == 0), stop=(t == 3))
             z2ps[k] = z2p
 
         def nega(k):
-            nc.scalar.copy(out=nega_all[:, 2 * k:2 * k + 2], in_=z2ps.pop(k)[:, :, 0])
+            z2p = z2ps.pop(k)
+            if on_vector(k):
+                nc.vector.tensor_reduce(out=nega_v[:, 2 * k:2 * k + 2], in_=z2p[:], axis=mybir.AxisListType.X,
+                                        op=ALU.add, negate=True)
+                return
+            for a in range(2):
+                n = 2 * k + a
+                njunk = work.tile([P, P], BF16, tag="njunk", bufs=2, name="njunk")
+                nc.scalar.activation(out=njunk[:], in_=z2p[:, a, :], func=ACT.Copy, scale=-1.0,
+                                     accum_out=nega_s[:, n:n + 1])
 
         def stt(k):
             u = work.tile([P, 2, NREF], F32, tag="u", bufs=2, name="u")
@@ -259,7 +279,7 @@ def tile_kernelloglikelihood_t_kernel(tc, x, pca_weight, pca_bias, X_ref, bandwi
             if a == 0:
                 ucls[k] = work.tile([P, 2, NREF], F32, tag="ucl", bufs=2, name="ucl")
             n = 2 * k + a
-            nc.vector.tensor_scalar(out=ucls[k][:, a, :], in0=us[k][:, a, :], scalar1=nega_all[:, n:n + 1], scalar2=None,
+            nc.vector.tensor_scalar(out=ucls[k][:, a, :], in0=us[k][:, a, :], scalar1=nega_of(k)[:, n:n + 1], scalar2=None,
                                     op0=ALU.max, op1=ALU.min, accum_out=mn_all[:, n:n + 1])
 
         def ex(k, a):
@@ -317,6 +337,9 @@ def tile_kernelloglikelihood_t_kernel(tc, x, pca_weight, pca_bias, X_ref, bandwi
         t1 = const.tile([P, NT], F32)
         nc.vector.tensor_tensor(out=t1[:], in0=lns[:], in1=mn_all[:], op=ALU.subtract)
         res = const.tile([P, NT], F32)
-        nc.vector.scalar_tensor_tensor(out=res[:], in0=t1[:], scalar=coeff[:, 0:1], in1=nega_all[:],
-                                       op0=ALU.add, op1=ALU.add)
+        for par, src in ((0, nega_v), (1, nega_s)):
+            def quad(ap):
+                return ap.rearrange("p (g q c) -> p g q c", q=2, c=2)[:, :, par, :]
+            nc.vector.scalar_tensor_tensor(out=quad(res[:]), in0=quad(t1[:]), scalar=coeff[:, 0:1], in1=quad(src[:]),
+                                           op0=ALU.add, op1=ALU.add)
         nc.sync.dma_start(out=out.rearrange("(p n) -> p n", n=NT), in_=res[:])

@@ -175,14 +175,7 @@ def tile_kernelloglikelihood_t_kernel(tc, x, pca_weight, pca_bias, X_ref, bandwi
 
         mn_all = const.tile([P, NT], F32)
         sum_all = const.tile([P, NT], F32)
-        nega_v = const.tile([P, NT], F32)
-        nega_s = const.tile([P, NT], F32)
-
-        def on_vector(k):
-            return k % 2 == 0
-
-        def nega_of(k):
-            return nega_v if on_vector(k) else nega_s
+        nega_all = const.tile([P, NT], F32)
 
         xcodes = {}
         zps = {}
@@ -258,15 +251,11 @@ def tile_kernelloglikelihood_t_kernel(tc, x, pca_weight, pca_bias, X_ref, bandwi
 
         def nega(k):
             z2p = z2ps.pop(k)
-            if on_vector(k):
-                nc.vector.tensor_reduce(out=nega_v[:, 2 * k:2 * k + 2], in_=z2p[:], axis=mybir.AxisListType.X,
-                                        op=ALU.add, negate=True)
-                return
             for a in range(2):
                 n = 2 * k + a
                 njunk = work.tile([P, P], BF16, tag="njunk", bufs=2, name="njunk")
                 nc.scalar.activation(out=njunk[:], in_=z2p[:, a, :], func=ACT.Copy, scale=-1.0,
-                                     accum_out=nega_s[:, n:n + 1])
+                                     accum_out=nega_all[:, n:n + 1])
 
         def stt(k):
             u = work.tile([P, 2, NREF], F32, tag="u", bufs=2, name="u")
@@ -279,7 +268,7 @@ def tile_kernelloglikelihood_t_kernel(tc, x, pca_weight, pca_bias, X_ref, bandwi
             if a == 0:
                 ucls[k] = work.tile([P, 2, NREF], F32, tag="ucl", bufs=2, name="ucl")
             n = 2 * k + a
-            nc.vector.tensor_scalar(out=ucls[k][:, a, :], in0=us[k][:, a, :], scalar1=nega_of(k)[:, n:n + 1], scalar2=None,
+            nc.vector.tensor_scalar(out=ucls[k][:, a, :], in0=us[k][:, a, :], scalar1=nega_all[:, n:n + 1], scalar2=None,
                                     op0=ALU.max, op1=ALU.min, accum_out=mn_all[:, n:n + 1])
 
         def ex(k, a):
@@ -337,9 +326,6 @@ def tile_kernelloglikelihood_t_kernel(tc, x, pca_weight, pca_bias, X_ref, bandwi
         t1 = const.tile([P, NT], F32)
         nc.vector.tensor_tensor(out=t1[:], in0=lns[:], in1=mn_all[:], op=ALU.subtract)
         res = const.tile([P, NT], F32)
-        for par, src in ((0, nega_v), (1, nega_s)):
-            def quad(ap):
-                return ap.rearrange("p (g q c) -> p g q c", q=2, c=2)[:, :, par, :]
-            nc.vector.scalar_tensor_tensor(out=quad(res[:]), in0=quad(t1[:]), scalar=coeff[:, 0:1], in1=quad(src[:]),
-                                           op0=ALU.add, op1=ALU.add)
+        nc.vector.scalar_tensor_tensor(out=res[:], in0=t1[:], scalar=coeff[:, 0:1], in1=nega_all[:],
+                                       op0=ALU.add, op1=ALU.add)
         nc.sync.dma_start(out=out.rearrange("(p n) -> p n", n=NT), in_=res[:])

@@ -23,7 +23,11 @@ NREF = 256
 NT = B // P
 NPAIR = NT // 2
 CHUNKS = (2, 2, 4, 8, 8, 8, 8, 8, 8, 8)
-PS_BUFS = {"xT": 2, "Z": 4, "G": 1, "z2": 1}
+PS_BUFS = {"xT": 1, "Z": 4, "G": 2, "z2": 1}
+
+
+def EV_ON_S(k, a):
+    return a == 1 and k % 2 == 1
 
 
 def tile_kernelloglikelihood_t_kernel(tc, x, pca_weight, pca_bias, X_ref, bandwidth, out):
@@ -85,7 +89,7 @@ def tile_kernelloglikelihood_t_kernel(tc, x, pca_weight, pca_bias, X_ref, bandwi
         wsc = const.tile([P, 4 * P], U8, align_bytes=64)
         w32 = wsb[:].bitcast(F32)
         for a in range(2):
-            transposes("w%d" % a, [w32[:, 2 * a + (i // 2), P * (i % 2):P * (i % 2) + P] for i in range(4)], "xT")
+            transposes("w%d" % a, [w32[:, 2 * a + (i // 2), P * (i % 2):P * (i % 2) + P] for i in range(4)], "Z")
         for a in range(2):
             copy_out("w%d" % a)
         for a in range(2):
@@ -107,8 +111,6 @@ def tile_kernelloglikelihood_t_kernel(tc, x, pca_weight, pca_bias, X_ref, bandwi
         nc.vector.reciprocal(out=rinv[:], in_=h32[:])
         rsq = small("rsq")
         nc.vector.tensor_scalar(out=rsq[:], in0=rinv[:], scalar1=math.sqrt(0.5), scalar2=None, op0=ALU.mult)
-        bsc = small("bsc", w=4)
-        nc.vector.tensor_scalar(out=bsc[:], in0=b32[:], scalar1=rsq[:, 0:1], scalar2=None, op0=ALU.mult)
 
         ei = small("ei", I32)
         mi = small("mi", I32)
@@ -179,6 +181,7 @@ def tile_kernelloglikelihood_t_kernel(tc, x, pca_weight, pca_bias, X_ref, bandwi
 
         xcodes = {}
         zps = {}
+        zfs = {}
         zgs = {}
         qts = {}
         zcodes = {}
@@ -212,17 +215,26 @@ def tile_kernelloglikelihood_t_kernel(tc, x, pca_weight, pca_bias, X_ref, bandwi
 
         def ev(k, a):
             if a == 0:
-                zgs[k] = work.tile([P, 2, P, 4], BF16, tag="zg", bufs=2, align_bytes=64, name="zg")
-            nc.vector.tensor_tensor(out=zgs[k][:, a, :, :], in0=zps[(k, a)][:].rearrange("p t i -> p i t"),
-                                    in1=b32[:].unsqueeze(1).to_broadcast([P, P, 4]), op=ALU.add)
+                zfs[k] = work.tile([P, 2, 4, P], F32, tag="zf", bufs=3, name="zf")
+            zp = zps.pop((k, a))
+            if EV_ON_S(k, a):
+                for t in range(4):
+                    nc.scalar.activation(out=zfs[k][:, a, t, :], in_=zp[:, t, :], func=ACT.Identity,
+                                         bias=b32[:, t:t + 1], scale=1.0)
+            else:
+                nc.vector.tensor_tensor(out=zfs[k][:, a, :, :], in0=zp[:],
+                                        in1=b32[:].unsqueeze(2).to_broadcast([P, 4, P]), op=ALU.add)
+
+        def cast(k):
+            zg = work.tile([P, 2, P, 4], BF16, tag="zg", bufs=2, align_bytes=64, name="zg")
+            nc.gpsimd.tensor_scalar(out=zg[:], in0=zfs[k][:].rearrange("p a t i -> p a i t"), scalar1=1.0, scalar2=0.0,
+                                    op0=ALU.mult, op1=ALU.add)
+            zgs[k] = zg
 
         def sq(k, a):
-            zp = zps.pop((k, a))
-            q = work.tile([P, 4, P], F32, tag="q", bufs=4, name="q")
-            for t in range(4):
-                nc.scalar.activation(out=q[:, t, :], in_=zp[:, t, :], func=ACT.Square, bias=bsc[:, t:t + 1],
-                                     scale=rsq[:, 0:1])
-            qts[(k, a)] = q
+            if a == 0:
+                qts[k] = work.tile([P, 2, 4, P], F32, tag="q", bufs=3, name="q")
+            nc.scalar.activation(out=qts[k][:, a, :, :], in_=zfs[k][:, a, :, :], func=ACT.Square, scale=rsq[:, 0:1])
 
         def q_z(k):
             zg = zgs.pop(k)
@@ -242,10 +254,10 @@ def tile_kernelloglikelihood_t_kernel(tc, x, pca_weight, pca_bias, X_ref, bandwi
 
         def z2(k):
             z2p = psum.tile([P, 2, P], F32, tag="z2", bufs=PS_BUFS["z2"], name="z2p")
+            q = qts.pop(k)
             for a in range(2):
-                q = qts.pop((k, a))
                 for t in range(4):
-                    nc.tensor.matmul(out=z2p[:, a, :], lhsT=q[:, t, :], rhs=identf[:], is_transpose=True,
+                    nc.tensor.matmul(out=z2p[:, a, :], lhsT=q[:, a, t, :], rhs=identf[:], is_transpose=True,
                                      start=(t == 0), stop=(t == 3))
             z2ps[k] = z2p
 
@@ -277,40 +289,45 @@ def tile_kernelloglikelihood_t_kernel(tc, x, pca_weight, pca_bias, X_ref, bandwi
             nc.scalar.activation(out=ejunk[:], in_=ucls[k][:, a, :], func=ACT.Exp, bias=mn_all[:, n:n + 1], scale=-1.0,
                                  accum_out=sum_all[:, n:n + 1])
 
-        for j in range(-3, NPAIR + 2):
+        for j in range(-3, NPAIR + 4):
+            if valid(j + 2):
+                copy_out(j + 2)
+            if j == -2:
+                transposes("r", [r32[:, i // 2, (i % 2):256:2] for i in range(4)], "Z")
+                copy_out("r")
+                r_squares()
+            if valid(j - 4):
+                ex(j - 4, 0)
+                ex(j - 4, 1)
             if valid(j + 1):
                 s1(j + 1)
             if valid(j - 1):
-                s2(j - 1)
                 z2(j - 1)
             if valid(j + 3):
                 t_x(j + 3)
-            if j == -2:
-                transposes("r", [r32[:, i // 2, (i % 2):256:2] for i in range(4)], "Z")
             if j == 0:
                 r2t = psum.tile([P, 2, P], F32, tag="G", bufs=PS_BUFS["G"], name="r2t")
                 for jt in range(2):
                     nc.tensor.transpose(r2t[:, jt, :], rep[:, jt, :], identf[:])
-            if valid(j + 2):
-                copy_out(j + 2)
-            if j == -2:
-                copy_out("r")
-                r_squares()
-            for a in range(2):
-                if valid(j):
-                    ev(j, a)
-                    sq(j, a)
-                if valid(j - 2):
-                    cm(j - 2, a)
-                    ex(j - 2, a)
+            if valid(j):
+                ev(j, 0)
+                ev(j, 1)
+                cast(j)
             if valid(j + 2):
                 q_x(j + 2)
             if j == -2:
                 quantise("r", rc[:], rsc[:])
             if valid(j - 1):
-                stt(j - 1)
+                q_z(j - 1)
+                s2(j - 1)
             if valid(j):
-                q_z(j)
+                sq(j, 0)
+                sq(j, 1)
+            if valid(j - 3):
+                cm(j - 3, 0)
+                cm(j - 3, 1)
+            if valid(j - 2):
+                stt(j - 2)
             if valid(j - 1):
                 nega(j - 1)
             if j == 0:

@@ -23,11 +23,7 @@ NREF = 256
 NT = B // P
 NPAIR = NT // 2
 CHUNKS = (2, 2, 4, 8, 8, 8, 8, 8, 8, 8)
-PS_BUFS = {"xT": 1, "Z": 4, "G": 2, "z2": 1}
-
-
-def EV_ON_S(k, a):
-    return a == 1 and k % 2 == 1
+PS_BUFS = {"xT": 1, "Z": 3, "G": 2, "ZT": 2}
 
 
 def tile_kernelloglikelihood_t_kernel(tc, x, pca_weight, pca_bias, X_ref, bandwidth, out):
@@ -43,7 +39,8 @@ def tile_kernelloglikelihood_t_kernel(tc, x, pca_weight, pca_bias, X_ref, bandwi
         bsb = const.tile([P, 4], BF16)
         nc.scalar.dma_start(out=bsb[:], in_=pca_bias.rearrange("(p t) -> p t", t=4))
         wsb = const.tile([P, 4, D], BF16)
-        nc.sync.dma_start(out=wsb[:], in_=pca_weight.rearrange("(p t) k -> p t k", t=4))
+        wv = pca_weight.rearrange("(p t) k -> p t k", t=4)
+        nc.sync.dma_start(out=wsb[:, 0:2, :], in_=wv[:, 0:2, :])
         xv = x.rearrange("(p n) k -> p n k", n=NT)
         xw = []
         n0 = 0
@@ -56,6 +53,8 @@ def tile_kernelloglikelihood_t_kernel(tc, x, pca_weight, pca_bias, X_ref, bandwi
                 xw.append(xt32[:, k, :])
             n0 += cn
             if ci == 0:
+                nc.sync.dma_start(out=wsb[:, 2:4, :], in_=wv[:, 2:4, :])
+            if ci == 1:
                 nc.sync.dma_start(out=rsb[:], in_=X_ref.rearrange("(p j) c -> p j c", j=2))
 
         identf = const.tile([P, P], F32)
@@ -74,11 +73,15 @@ def tile_kernelloglikelihood_t_kernel(tc, x, pca_weight, pca_bias, X_ref, bandwi
                     nc.tensor.transpose(tp[:, a, u, :], srcs[2 * a + u], identf[:])
             tps[key] = tp
 
-        def copy_out(key):
+        def copy_out(key, on_vector=False):
             tp = tps.pop(key)
             grouped = work.tile([P, 2 * P * 4], BF16, tag="grouped", bufs=3, align_bytes=64, name="grouped")
-            nc.scalar.copy(out=grouped[:].bitcast(F32).rearrange("p (a i u) -> p a i u", a=2, u=2),
-                           in_=tp[:].rearrange("p a u i -> p a i u"))
+            dst = grouped[:].bitcast(F32).rearrange("p (a i u) -> p a i u", a=2, u=2)
+            src = tp[:].rearrange("p a u i -> p a i u")
+            if on_vector:
+                nc.vector.tensor_copy(out=dst, in_=src)
+            else:
+                nc.scalar.copy(out=dst, in_=src)
             groupeds[key] = grouped
 
         def quantise(key, codes, scales):
@@ -88,12 +91,33 @@ def tile_kernelloglikelihood_t_kernel(tc, x, pca_weight, pca_bias, X_ref, bandwi
         wc = const.tile([P, 4 * P], U32, align_bytes=64)
         wsc = const.tile([P, 4 * P], U8, align_bytes=64)
         w32 = wsb[:].bitcast(F32)
-        for a in range(2):
+
+        def t_w(a):
             transposes("w%d" % a, [w32[:, 2 * a + (i // 2), P * (i % 2):P * (i % 2) + P] for i in range(4)], "Z")
-        for a in range(2):
-            copy_out("w%d" % a)
-        for a in range(2):
+
+        def q_w(a):
             quantise("w%d" % a, wc[:, 256 * a:256 * a + 256], wsc[:, 256 * a:256 * a + 256])
+
+        xcodes = {}
+
+        def t_x(k):
+            transposes(k, [xw[2 * k + (i // 2)][:, P * (i % 2):P * (i % 2) + P] for i in range(4)], "xT")
+
+        def q_x(k):
+            xc = work.tile([P, 2 * P], U32, tag="xc", bufs=4, align_bytes=64, name="xc")
+            xs = work.tile([P, 2 * P], U8, tag="xs", bufs=4, align_bytes=64, name="xs")
+            quantise(k, xc[:], xs[:])
+            xcodes[k] = (xc, xs)
+
+        t_w(0)
+        copy_out("w0")
+        t_x(0)
+        copy_out(0)
+        t_w(1)
+        q_w(0)
+        copy_out("w1", on_vector=True)
+        q_x(0)
+        q_w(1)
 
         h32 = small("h32")
         nc.vector.tensor_copy(out=h32[:], in_=hb[:])
@@ -142,48 +166,46 @@ def tile_kernelloglikelihood_t_kernel(tc, x, pca_weight, pca_bias, X_ref, bandwi
         ]
         coeff = small("coeff")
 
-        def ln_series():
-            w2 = small("w2")
-            nc.gpsimd.tensor_tensor(out=w2[:], in0=wq[:], in1=wq[:], op=ALU.mult)
-            poly = small("poly0")
-            nc.gpsimd.tensor_scalar(out=poly[:], in0=w2[:], scalar1=1.0 / 17.0, scalar2=1.0 / 15.0,
-                                    op0=ALU.mult, op1=ALU.add)
-            for odd in (13, 11, 9, 7, 5, 3, 1):
-                nxt = small("poly%d" % odd)
-                nc.gpsimd.tensor_scalar(out=nxt[:], in0=poly[:], scalar1=w2[:, 0:1], scalar2=1.0 / odd,
-                                        op0=ALU.mult, op1=ALU.add)
-                poly = nxt
-            wp = small("wp")
-            nc.gpsimd.tensor_tensor(out=wp[:], in0=poly[:], in1=wq[:], op=ALU.mult)
-            c1 = small("c1")
-            nc.gpsimd.tensor_scalar(out=c1[:], in0=e3[:], scalar1=-DC * math.log(2.0),
-                                    scalar2=-math.log(NREF) - 0.5 * DC * math.log(2.0 * math.pi),
-                                    op0=ALU.mult, op1=ALU.add)
-            nc.gpsimd.tensor_scalar(out=coeff[:], in0=wp[:], scalar1=-2.0 * DC, scalar2=c1[:, 0:1],
-                                    op0=ALU.mult, op1=ALU.add)
+        w2 = small("w2")
+        polys = [small("poly%d" % i) for i in range(8)]
+        wp = small("wp")
+        c1 = small("c1")
+
+        def horner(i, odd):
+            return lambda: nc.gpsimd.tensor_scalar(out=polys[i][:], in0=polys[i - 1][:], scalar1=w2[:, 0:1],
+                                                   scalar2=1.0 / odd, op0=ALU.mult, op1=ALU.add)
+
+        series_steps = [
+            lambda: nc.gpsimd.tensor_tensor(out=w2[:], in0=wq[:], in1=wq[:], op=ALU.mult),
+            lambda: nc.gpsimd.tensor_scalar(out=polys[0][:], in0=w2[:], scalar1=1.0 / 17.0, scalar2=1.0 / 15.0,
+                                            op0=ALU.mult, op1=ALU.add),
+        ] + [horner(i + 1, odd) for i, odd in enumerate((13, 11, 9, 7, 5, 3, 1))] + [
+            lambda: nc.gpsimd.tensor_tensor(out=wp[:], in0=polys[7][:], in1=wq[:], op=ALU.mult),
+            lambda: nc.gpsimd.tensor_scalar(out=c1[:], in0=e3[:], scalar1=-DC * math.log(2.0),
+                                            scalar2=-math.log(NREF) - 0.5 * DC * math.log(2.0 * math.pi),
+                                            op0=ALU.mult, op1=ALU.add),
+            lambda: nc.gpsimd.tensor_scalar(out=coeff[:], in0=wp[:], scalar1=-2.0 * DC, scalar2=c1[:, 0:1],
+                                            op0=ALU.mult, op1=ALU.add),
+        ]
 
         rc = const.tile([P, NREF], U32, align_bytes=64)
         rsc = const.tile([P, NREF], U8, align_bytes=64)
         r32 = rsb[:].bitcast(F32)
         r2 = small("r2", w=2)
-        rep = const.tile([P, 2, P], F32)
         csb = const.tile([P, NREF], F32)
 
-        def r_squares():
-            for jt in range(2):
-                rjunk = work.tile([P, DC], BF16, tag="rjunk", bufs=2, name="rjunk")
-                nc.scalar.activation(out=rjunk[:], in_=rsb[:, jt, :], func=ACT.Square, accum_out=r2[:, jt:jt + 1])
-                nc.gpsimd.tensor_copy(out=rep[:, jt, :], in_=r2[:, jt:jt + 1].to_broadcast([P, P]))
+        def r_square(jt):
+            rjunk = work.tile([P, DC], BF16, tag="rjunk", bufs=2, name="rjunk")
+            nc.scalar.activation(out=rjunk[:], in_=rsb[:, jt, :], func=ACT.Square, accum_out=r2[:, jt:jt + 1])
 
         mn_all = const.tile([P, NT], F32)
         sum_all = const.tile([P, NT], F32)
         nega_all = const.tile([P, NT], F32)
+        a_all = const.tile([P, NT], F32)
 
-        xcodes = {}
         zps = {}
         zfs = {}
         zgs = {}
-        qts = {}
         zcodes = {}
         z2ps = {}
         gps = {}
@@ -193,48 +215,41 @@ def tile_kernelloglikelihood_t_kernel(tc, x, pca_weight, pca_bias, X_ref, bandwi
         def valid(k):
             return 0 <= k < NPAIR
 
-        def t_x(k):
-            transposes(k, [xw[2 * k + (i // 2)][:, P * (i % 2):P * (i % 2) + P] for i in range(4)], "xT")
+        def s1(k, h):
+            xc, xs = xcodes[k]
+            zp = psum.tile([P, 2, 2 * P], F32, tag="Z", bufs=PS_BUFS["Z"], name="zp")
+            for tt in range(2):
+                t = 2 * h + tt
+                nc.tensor.matmul_mx(out=zp[:, tt, :],
+                                    lhsT=wc[:, P * t:P * t + P].bitcast(FP8X4), lhsT_scale=wsc[:, P * t:P * t + P],
+                                    rhs=xc[:].bitcast(FP8X4), rhs_scale=xs[:], start=True, stop=True)
+            zps[(k, h)] = zp
 
-        def q_x(k):
-            xc = work.tile([P, 2 * P], U32, tag="xc", bufs=3, align_bytes=64, name="xc")
-            xs = work.tile([P, 2 * P], U8, tag="xs", bufs=3, align_bytes=64, name="xs")
-            quantise(k, xc[:], xs[:])
-            xcodes[k] = (xc, xs)
+        def plane(k):
+            zfs[k] = work.tile([P, 4, 2 * P], F32, tag="zf", bufs=3, name="zf")
+            nc.scalar.activation(out=zfs[k][:, 3, :], in_=zps[(k, 1)][:, 1, :], func=ACT.Identity,
+                                 bias=b32[:, 3:4], scale=1.0)
 
-        def s1(k):
-            xc, xs = xcodes.pop(k)
-            for a in range(2):
-                zp = psum.tile([P, 4, P], F32, tag="Z", bufs=PS_BUFS["Z"], name="zp")
-                for t in range(4):
-                    nc.tensor.matmul_mx(out=zp[:, t, :],
-                                        lhsT=wc[:, P * t:P * t + P].bitcast(FP8X4), lhsT_scale=wsc[:, P * t:P * t + P],
-                                        rhs=xc[:, P * a:P * a + P].bitcast(FP8X4), rhs_scale=xs[:, P * a:P * a + P],
-                                        start=True, stop=True)
-                zps[(k, a)] = zp
-
-        def ev(k, a):
-            if a == 0:
-                zfs[k] = work.tile([P, 2, 4, P], F32, tag="zf", bufs=3, name="zf")
-            zp = zps.pop((k, a))
-            if EV_ON_S(k, a):
-                for t in range(4):
-                    nc.scalar.activation(out=zfs[k][:, a, t, :], in_=zp[:, t, :], func=ACT.Identity,
-                                         bias=b32[:, t:t + 1], scale=1.0)
+        def ev(k, h):
+            zp = zps.pop((k, h))
+            if h == 0:
+                nc.vector.tensor_tensor(out=zfs[k][:, 0:2, :], in0=zp[:],
+                                        in1=b32[:, 0:2].unsqueeze(2).to_broadcast([P, 2, 2 * P]), op=ALU.add)
             else:
-                nc.vector.tensor_tensor(out=zfs[k][:, a, :, :], in0=zp[:],
-                                        in1=b32[:].unsqueeze(2).to_broadcast([P, 4, P]), op=ALU.add)
+                nc.vector.tensor_scalar(out=zfs[k][:, 2, :], in0=zp[:, 0, :], scalar1=b32[:, 2:3], scalar2=None,
+                                        op0=ALU.add)
 
         def cast(k):
-            zg = work.tile([P, 2, P, 4], BF16, tag="zg", bufs=2, align_bytes=64, name="zg")
-            nc.gpsimd.tensor_scalar(out=zg[:], in0=zfs[k][:].rearrange("p a t i -> p a i t"), scalar1=1.0, scalar2=0.0,
-                                    op0=ALU.mult, op1=ALU.add)
+            zg = work.tile([P, 2, P, 4], BF16, tag="zg", bufs=1, align_bytes=64, name="zg")
+            nc.gpsimd.tensor_scalar(out=zg[:], in0=zfs[k][:].rearrange("p t (a i) -> p a i t", a=2), scalar1=1.0,
+                                    scalar2=0.0, op0=ALU.mult, op1=ALU.add)
             zgs[k] = zg
 
         def sq(k, a):
-            if a == 0:
-                qts[k] = work.tile([P, 2, 4, P], F32, tag="q", bufs=3, name="q")
-            nc.scalar.activation(out=qts[k][:, a, :, :], in_=zfs[k][:, a, :, :], func=ACT.Square, scale=rsq[:, 0:1])
+            n = 2 * k + a
+            sjunk = work.tile([P, 4 * P], BF16, tag="sjunk", bufs=2, name="sjunk")
+            nc.scalar.activation(out=sjunk[:], in_=z2ps.pop((k, a))[:].rearrange("p t c -> p (t c)"), func=ACT.Square,
+                                 scale=rsq[:, 0:1], accum_out=a_all[:, n:n + 1])
 
         def q_z(k):
             zg = zgs.pop(k)
@@ -253,21 +268,16 @@ def tile_kernelloglikelihood_t_kernel(tc, x, pca_weight, pca_bias, X_ref, bandwi
             gps[k] = gp
 
         def z2(k):
-            z2p = psum.tile([P, 2, P], F32, tag="z2", bufs=PS_BUFS["z2"], name="z2p")
-            q = qts.pop(k)
+            zf = zfs.pop(k)
             for a in range(2):
+                ztp = psum.tile([P, 4, P], F32, tag="ZT", bufs=PS_BUFS["ZT"], name="ztp")
                 for t in range(4):
-                    nc.tensor.matmul(out=z2p[:, a, :], lhsT=q[:, a, t, :], rhs=identf[:], is_transpose=True,
-                                     start=(t == 0), stop=(t == 3))
-            z2ps[k] = z2p
+                    nc.tensor.transpose(ztp[:, t, :], zf[:, t, P * a:P * a + P], identf[:])
+                z2ps[(k, a)] = ztp
 
         def nega(k):
-            z2p = z2ps.pop(k)
-            for a in range(2):
-                n = 2 * k + a
-                njunk = work.tile([P, P], BF16, tag="njunk", bufs=2, name="njunk")
-                nc.scalar.activation(out=njunk[:], in_=z2p[:, a, :], func=ACT.Copy, scale=-1.0,
-                                     accum_out=nega_all[:, n:n + 1])
+            nc.scalar.activation(out=nega_all[:, 2 * k:2 * k + 2], in_=a_all[:, 2 * k:2 * k + 2], func=ACT.Copy,
+                                 scale=-1.0)
 
         def stt(k):
             u = work.tile([P, 2, NREF], F32, tag="u", bufs=2, name="u")
@@ -278,7 +288,7 @@ def tile_kernelloglikelihood_t_kernel(tc, x, pca_weight, pca_bias, X_ref, bandwi
 
         def cm(k, a):
             if a == 0:
-                ucls[k] = work.tile([P, 2, NREF], F32, tag="ucl", bufs=2, name="ucl")
+                ucls[k] = work.tile([P, 2, NREF], F32, tag="ucl", bufs=4, name="ucl")
             n = 2 * k + a
             nc.vector.tensor_scalar(out=ucls[k][:, a, :], in0=us[k][:, a, :], scalar1=nega_all[:, n:n + 1], scalar2=None,
                                     op0=ALU.max, op1=ALU.min, accum_out=mn_all[:, n:n + 1])
@@ -289,60 +299,99 @@ def tile_kernelloglikelihood_t_kernel(tc, x, pca_weight, pca_bias, X_ref, bandwi
             nc.scalar.activation(out=ejunk[:], in_=ucls[k][:, a, :], func=ACT.Exp, bias=mn_all[:, n:n + 1], scale=-1.0,
                                  accum_out=sum_all[:, n:n + 1])
 
-        for j in range(-3, NPAIR + 4):
-            if valid(j + 2):
-                copy_out(j + 2)
-            if j == -2:
-                transposes("r", [r32[:, i // 2, (i % 2):256:2] for i in range(4)], "Z")
-                copy_out("r")
-                r_squares()
-            if valid(j - 4):
-                ex(j - 4, 0)
-                ex(j - 4, 1)
+        LN0 = 3
+        SER0 = LN0 + len(ln_steps) + 1
+        def x_steps(j):
+            if j == -1:
+                return [1]
+            if j == 0:
+                return [2, 3]
+            return [j + 3] if 1 <= j and j + 3 < NPAIR else []
+
+        def x_step(k):
+            copy_out(k)
+            if k + 1 < NPAIR:
+                t_x(k + 1)
+
+        def cms(k):
+            if valid(k):
+                cm(k, 0)
+                cm(k, 1)
+
+        t_x(1)
+        for j in range(-1, NPAIR + 5):
+            xs_now = x_steps(j)
             if valid(j + 1):
-                s1(j + 1)
+                s1(j + 1, 0)
             if valid(j - 1):
                 z2(j - 1)
-            if valid(j + 3):
-                t_x(j + 3)
-            if j == 0:
+            if xs_now:
+                x_step(xs_now[0])
+            if j == 1:
                 r2t = psum.tile([P, 2, P], F32, tag="G", bufs=PS_BUFS["G"], name="r2t")
                 for jt in range(2):
-                    nc.tensor.transpose(r2t[:, jt, :], rep[:, jt, :], identf[:])
+                    nc.tensor.matmul(out=r2t[:, jt, :], lhsT=r2[:, jt:jt + 1].to_broadcast([P, P]), rhs=identf[:],
+                                     start=True, stop=True)
             if valid(j):
+                plane(j)
                 ev(j, 0)
-                ev(j, 1)
-                cast(j)
-            if valid(j + 2):
-                q_x(j + 2)
-            if j == -2:
-                quantise("r", rc[:], rsc[:])
-            if valid(j - 1):
-                q_z(j - 1)
-                s2(j - 1)
+            if valid(j + 1):
+                s1(j + 1, 1)
+            for k in xs_now[1:]:
+                x_step(k)
             if valid(j):
-                sq(j, 0)
-                sq(j, 1)
-            if valid(j - 3):
-                cm(j - 3, 0)
-                cm(j - 3, 1)
-            if valid(j - 2):
+                ev(j, 1)
+            if j < NPAIR:
+                if valid(j - 3):
+                    stt(j - 3)
+                cms(j - 4)
+            for k in xs_now:
+                q_x(k)
+            if j == NPAIR:
+                stt(j - 3)
+                cms(j - 4)
+                s2(j - 2)
                 stt(j - 2)
             if valid(j - 1):
-                nega(j - 1)
+                q_z(j - 1)
+            if j < NPAIR and valid(j - 2):
+                s2(j - 2)
+            if j == NPAIR + 1:
+                s2(j - 2)
+                cms(j - 4)
+                stt(j - 2)
+                cms(j - 3)
+                cms(j - 2)
+            if j == 1:
+                quantise("r", rc[:], rsc[:])
+            if LN0 <= j < LN0 + len(ln_steps):
+                ln_steps[j - LN0]()
+            if SER0 <= j < SER0 + len(series_steps):
+                series_steps[j - SER0]()
+            if valid(j):
+                cast(j)
+            if j == -1:
+                r_square(0)
+                transposes("r", [r32[:, i // 2, (i % 2):256:2] for i in range(4)], "G")
             if j == 0:
+                r_square(1)
+                copy_out("r")
+            if j == 1:
                 nc.scalar.activation(out=csb[:], in_=r2t[:].rearrange("p a j -> p (a j)"), func=ACT.Copy,
                                      scale=s_ap[:, 0:1])
-            if 3 <= j < 3 + len(ln_steps):
-                ln_steps[j - 3]()
-            if j == 3 + len(ln_steps):
-                ln_series()
+            if valid(j - 5):
+                ex(j - 5, 0)
+                ex(j - 5, 1)
+            if valid(j - 1):
+                sq(j - 1, 0)
+                sq(j - 1, 1)
+                nega(j - 1)
 
+        base = const.tile([P, NT], F32)
+        nc.vector.scalar_tensor_tensor(out=base[:], in0=nega_all[:], scalar=coeff[:, 0:1], in1=mn_all[:],
+                                       op0=ALU.add, op1=ALU.subtract)
         lns = const.tile([P, NT], F32)
         nc.scalar.activation(out=lns[:], in_=sum_all[:], func=ACT.Ln)
-        t1 = const.tile([P, NT], F32)
-        nc.vector.tensor_tensor(out=t1[:], in0=lns[:], in1=mn_all[:], op=ALU.subtract)
         res = const.tile([P, NT], F32)
-        nc.vector.scalar_tensor_tensor(out=res[:], in0=t1[:], scalar=coeff[:, 0:1], in1=nega_all[:],
-                                       op0=ALU.add, op1=ALU.add)
+        nc.vector.tensor_tensor(out=res[:], in0=lns[:], in1=base[:], op=ALU.add)
         nc.sync.dma_start(out=out.rearrange("(p n) -> p n", n=NT), in_=res[:])

@@ -276,7 +276,7 @@ def tile_kernelloglikelihood_t_kernel(tc, x, pca_weight, pca_bias, X_ref, bandwi
                 z2ps[(k, a)] = ztp
 
         def nega(k):
-            nc.scalar.activation(out=nega_all[:, 2 * k:2 * k + 2], in_=a_all[:, 2 * k:2 * k + 2], func=ACT.Copy,
+            nc.scalar.activation(out=nega_all[:, 2 * k - 2:2 * k + 2], in_=a_all[:, 2 * k - 2:2 * k + 2], func=ACT.Copy,
                                  scale=-1.0)
 
         def stt(k):
@@ -379,13 +379,16 @@ def tile_kernelloglikelihood_t_kernel(tc, x, pca_weight, pca_bias, X_ref, bandwi
             if j == 1:
                 nc.scalar.activation(out=csb[:], in_=r2t[:].rearrange("p a j -> p (a j)"), func=ACT.Copy,
                                      scale=s_ap[:, 0:1])
+            if valid(j - 2) and j % 2 == 1 and j < NPAIR:
+                nega(j - 2)
             if valid(j - 5):
                 ex(j - 5, 0)
                 ex(j - 5, 1)
             if valid(j - 1):
                 sq(j - 1, 0)
                 sq(j - 1, 1)
-                nega(j - 1)
+                if j == NPAIR:
+                    nega(j - 1)
 
         base = const.tile([P, NT], F32)
         nc.vector.scalar_tensor_tensor(out=base[:], in0=nega_all[:], scalar=coeff[:, 0:1], in1=mn_all[:],

@@ -22,7 +22,7 @@ DC = 512
 NREF = 256
 NT = B // P
 NPAIR = NT // 2
-CHUNKS = (2, 2, 4, 8, 8, 8, 8, 8, 8, 8)
+CHUNKS = (2, 2, 4, 4, 4, 8, 8, 8, 8, 8, 8)
 PS_BUFS = {"xT": 1, "Z": 3, "G": 2, "ZT": 2}
 
 
@@ -54,7 +54,7 @@ def tile_kernelloglikelihood_t_kernel(tc, x, pca_weight, pca_bias, X_ref, bandwi
             n0 += cn
             if ci == 0:
                 nc.sync.dma_start(out=wsb[:, 2:4, :], in_=wv[:, 2:4, :])
-            if ci == 1:
+            if ci == 2:
                 nc.sync.dma_start(out=rsb[:], in_=X_ref.rearrange("(p j) c -> p j c", j=2))
 
         identf = const.tile([P, P], F32)
@@ -100,41 +100,41 @@ def tile_kernelloglikelihood_t_kernel(tc, x, pca_weight, pca_bias, X_ref, bandwi
 
         xcodes = {}
 
-        def t_x(k):
-            transposes(k, [xw[2 * k + (i // 2)][:, P * (i % 2):P * (i % 2) + P] for i in range(4)], "xT")
+        def t_x(k, tag="xT"):
+            transposes(k, [xw[2 * k + (i // 2)][:, P * (i % 2):P * (i % 2) + P] for i in range(4)], tag)
 
         def q_x(k):
-            xc = work.tile([P, 2 * P], U32, tag="xc", bufs=4, align_bytes=64, name="xc")
-            xs = work.tile([P, 2 * P], U8, tag="xs", bufs=4, align_bytes=64, name="xs")
+            xc = work.tile([P, 2 * P], U32, tag="xc", bufs=8, align_bytes=64, name="xc")
+            xs = work.tile([P, 2 * P], U8, tag="xs", bufs=8, align_bytes=64, name="xs")
             quantise(k, xc[:], xs[:])
             xcodes[k] = (xc, xs)
 
-        t_w(0)
-        copy_out("w0")
-        t_x(0)
-        copy_out(0)
-        t_w(1)
-        q_w(0)
-        copy_out("w1", on_vector=True)
-        q_x(0)
-        q_w(1)
-
         h32 = small("h32")
-        nc.vector.tensor_copy(out=h32[:], in_=hb[:])
-        hh = small("hh")
-        nc.vector.tensor_tensor(out=hh[:], in0=h32[:], in1=h32[:], op=ALU.mult)
-        rh = small("rh")
-        nc.vector.reciprocal(out=rh[:], in_=hh[:])
-        n2s = small("n2s")
-        nc.vector.tensor_scalar(out=n2s[:], in0=rh[:], scalar1=-1.0, scalar2=None, op0=ALU.mult)
-        s_ap = small("s_ap")
-        nc.vector.tensor_scalar(out=s_ap[:], in0=rh[:], scalar1=0.5, scalar2=None, op0=ALU.mult)
         b32 = small("b32", w=4)
-        nc.vector.tensor_copy(out=b32[:], in_=bsb[:])
+        hh = small("hh")
+        rh = small("rh")
         rinv = small("rinv")
-        nc.vector.reciprocal(out=rinv[:], in_=h32[:])
+        n2s = small("n2s")
+        s_ap = small("s_ap")
         rsq = small("rsq")
+        t_w(0)
+        t_x(0)
+        t_w(1)
+        t_x(1, "ZT")
+        copy_out("w0", on_vector=True)
+        copy_out(0)
+        copy_out("w1")
+        nc.vector.tensor_copy(out=h32[:], in_=hb[:])
+        nc.vector.tensor_copy(out=b32[:], in_=bsb[:])
+        q_w(0)
+        nc.vector.tensor_tensor(out=hh[:], in0=h32[:], in1=h32[:], op=ALU.mult)
+        nc.vector.reciprocal(out=rinv[:], in_=h32[:])
+        q_x(0)
+        nc.vector.reciprocal(out=rh[:], in_=hh[:])
         nc.vector.tensor_scalar(out=rsq[:], in0=rinv[:], scalar1=math.sqrt(0.5), scalar2=None, op0=ALU.mult)
+        q_w(1)
+        nc.vector.tensor_scalar(out=n2s[:], in0=rh[:], scalar1=-1.0, scalar2=None, op0=ALU.mult)
+        nc.vector.tensor_scalar(out=s_ap[:], in0=rh[:], scalar1=0.5, scalar2=None, op0=ALU.mult)
 
         ei = small("ei", I32)
         mi = small("mi", I32)
@@ -143,6 +143,7 @@ def tile_kernelloglikelihood_t_kernel(tc, x, pca_weight, pca_bias, X_ref, bandwi
         halve = small("halve")
         m2 = small("m2")
         e3 = small("e3")
+        num = small("num")
         den = small("den")
         rden = small("rden")
         wq = small("wq")
@@ -154,15 +155,15 @@ def tile_kernelloglikelihood_t_kernel(tc, x, pca_weight, pca_bias, X_ref, bandwi
                                             scalar2=0x3F800000, op0=ALU.bitwise_and, op1=ALU.bitwise_or),
             lambda: nc.vector.tensor_copy(out=ef[:], in_=ei[:]),
             lambda: nc.vector.tensor_single_scalar(out=gt[:], in_=mant, scalar=math.sqrt(2.0), op=ALU.is_gt),
-            lambda: nc.vector.tensor_scalar(out=halve[:], in0=gt[:], scalar1=-0.5, scalar2=1.0,
+            lambda: nc.gpsimd.tensor_scalar(out=halve[:], in0=gt[:], scalar1=-0.5, scalar2=1.0,
                                             op0=ALU.mult, op1=ALU.add),
-            lambda: nc.vector.tensor_tensor(out=m2[:], in0=mant, in1=halve[:], op=ALU.mult),
-            lambda: nc.vector.scalar_tensor_tensor(out=e3[:], in0=ef[:], scalar=-127.0, in1=gt[:],
-                                                   op0=ALU.add, op1=ALU.add),
-            lambda: nc.vector.tensor_scalar(out=den[:], in0=m2[:], scalar1=1.0, scalar2=None, op0=ALU.add),
+            lambda: nc.gpsimd.tensor_tensor(out=m2[:], in0=mant, in1=halve[:], op=ALU.mult),
+            lambda: nc.gpsimd.tensor_scalar(out=e3[:], in0=ef[:], scalar1=-127.0, scalar2=gt[:, 0:1],
+                                            op0=ALU.add, op1=ALU.add),
+            lambda: nc.gpsimd.tensor_scalar(out=num[:], in0=m2[:], scalar1=-1.0, scalar2=None, op0=ALU.add),
+            lambda: nc.gpsimd.tensor_scalar(out=den[:], in0=m2[:], scalar1=1.0, scalar2=None, op0=ALU.add),
             lambda: nc.vector.reciprocal(out=rden[:], in_=den[:]),
-            lambda: nc.vector.scalar_tensor_tensor(out=wq[:], in0=m2[:], scalar=-1.0, in1=rden[:],
-                                                   op0=ALU.add, op1=ALU.mult),
+            lambda: nc.gpsimd.tensor_tensor(out=wq[:], in0=num[:], in1=rden[:], op=ALU.mult),
         ]
         coeff = small("coeff")
 
@@ -227,15 +228,18 @@ def tile_kernelloglikelihood_t_kernel(tc, x, pca_weight, pca_bias, X_ref, bandwi
 
         def plane(k):
             zfs[k] = work.tile([P, 4, 2 * P], F32, tag="zf", bufs=3, name="zf")
-            nc.scalar.activation(out=zfs[k][:, 3, :], in_=zps[(k, 1)][:, 1, :], func=ACT.Identity,
-                                 bias=b32[:, 3:4], scale=1.0)
+            if k < 5:
+                return
+            for t in ((2, 3) if k >= 27 else (3,)):
+                nc.scalar.activation(out=zfs[k][:, t, :], in_=zps[(k, 1)][:, t - 2, :], func=ACT.Identity,
+                                     bias=b32[:, t:t + 1], scale=1.0)
 
         def ev(k, h):
             zp = zps.pop((k, h))
-            if h == 0:
-                nc.vector.tensor_tensor(out=zfs[k][:, 0:2, :], in0=zp[:],
-                                        in1=b32[:, 0:2].unsqueeze(2).to_broadcast([P, 2, 2 * P]), op=ALU.add)
-            else:
+            if h == 0 or k < 5:
+                nc.vector.tensor_tensor(out=zfs[k][:, 2 * h:2 * h + 2, :], in0=zp[:],
+                                        in1=b32[:, 2 * h:2 * h + 2].unsqueeze(2).to_broadcast([P, 2, 2 * P]), op=ALU.add)
+            elif not (k >= 27):
                 nc.vector.tensor_scalar(out=zfs[k][:, 2, :], in0=zp[:, 0, :], scalar1=b32[:, 2:3], scalar2=None,
                                         op0=ALU.add)
 
@@ -301,16 +305,14 @@ def tile_kernelloglikelihood_t_kernel(tc, x, pca_weight, pca_bias, X_ref, bandwi
 
         LN0 = 3
         SER0 = LN0 + len(ln_steps) + 1
+
         def x_steps(j):
-            if j == -1:
-                return [1]
-            if j == 0:
-                return [2, 3]
-            return [j + 3] if 1 <= j and j + 3 < NPAIR else []
+            first = {1: 3, 2: 5}.get(j, j + 4)
+            return [k for k in ([first, first + 1] if j < 3 else [first]) if k < NPAIR]
 
         def x_step(k):
-            copy_out(k)
-            if k + 1 < NPAIR:
+            copy_out(k, on_vector=k in (3, 5))
+            if k + 1 < NPAIR and k + 1 != 4:
                 t_x(k + 1)
 
         def cms(k):
@@ -318,8 +320,26 @@ def tile_kernelloglikelihood_t_kernel(tc, x, pca_weight, pca_bias, X_ref, bandwi
                 cm(k, 0)
                 cm(k, 1)
 
-        t_x(1)
-        for j in range(-1, NPAIR + 5):
+        s1(0, 0)
+        copy_out(1)
+        t_x(2, "ZT")
+        s1(0, 1)
+        q_x(1)
+        r_square(0)
+        s1(1, 0)
+        plane(0)
+        ev(0, 0)
+        copy_out(2)
+        s1(1, 1)
+        ev(0, 1)
+        t_x(3)
+        q_x(2)
+        cast(0)
+        transposes("r", [r32[:, i // 2, (i % 2):256:2] for i in range(4)], "G")
+        t_x(4, "G")
+        r_square(1)
+        copy_out("r")
+        for j in range(1, NPAIR + 5):
             xs_now = x_steps(j)
             if valid(j + 1):
                 s1(j + 1, 0)
@@ -370,12 +390,6 @@ def tile_kernelloglikelihood_t_kernel(tc, x, pca_weight, pca_bias, X_ref, bandwi
                 series_steps[j - SER0]()
             if valid(j):
                 cast(j)
-            if j == -1:
-                r_square(0)
-                transposes("r", [r32[:, i // 2, (i % 2):256:2] for i in range(4)], "G")
-            if j == 0:
-                r_square(1)
-                copy_out("r")
             if j == 1:
                 nc.scalar.activation(out=csb[:], in_=r2t[:].rearrange("p a j -> p (a j)"), func=ACT.Copy,
                                      scale=s_ap[:, 0:1])

@@ -115,6 +115,7 @@ def tile_kernelloglikelihood_t_kernel(tc, x, pca_weight, pca_bias, X_ref, bandwi
         rh = small("rh")
         rinv = small("rinv")
         n2s = small("n2s")
+        ns_ap = small("ns_ap")
         s_ap = small("s_ap")
         rsq = small("rsq")
         t_w(0)
@@ -135,6 +136,7 @@ def tile_kernelloglikelihood_t_kernel(tc, x, pca_weight, pca_bias, X_ref, bandwi
         q_w(1)
         nc.vector.tensor_scalar(out=n2s[:], in0=rh[:], scalar1=-1.0, scalar2=None, op0=ALU.mult)
         nc.vector.tensor_scalar(out=s_ap[:], in0=rh[:], scalar1=0.5, scalar2=None, op0=ALU.mult)
+        nc.vector.tensor_scalar(out=ns_ap[:], in0=rh[:], scalar1=-0.5, scalar2=None, op0=ALU.mult)
 
         ei = small("ei", I32)
         mi = small("mi", I32)
@@ -230,7 +232,7 @@ def tile_kernelloglikelihood_t_kernel(tc, x, pca_weight, pca_bias, X_ref, bandwi
             zfs[k] = work.tile([P, 4, 2 * P], F32, tag="zf", bufs=3, name="zf")
             if k < 5:
                 return
-            for t in ((2, 3) if k >= 27 else (3,)):
+            for t in ((2, 3) if k >= 25 or k % 4 != 2 else (3,)):
                 nc.scalar.activation(out=zfs[k][:, t, :], in_=zps[(k, 1)][:, t - 2, :], func=ACT.Identity,
                                      bias=b32[:, t:t + 1], scale=1.0)
 
@@ -239,7 +241,7 @@ def tile_kernelloglikelihood_t_kernel(tc, x, pca_weight, pca_bias, X_ref, bandwi
             if h == 0 or k < 5:
                 nc.vector.tensor_tensor(out=zfs[k][:, 2 * h:2 * h + 2, :], in0=zp[:],
                                         in1=b32[:, 2 * h:2 * h + 2].unsqueeze(2).to_broadcast([P, 2, 2 * P]), op=ALU.add)
-            elif not (k >= 27):
+            elif not (k >= 25 or k % 4 != 2):
                 nc.vector.tensor_scalar(out=zfs[k][:, 2, :], in0=zp[:, 0, :], scalar1=b32[:, 2:3], scalar2=None,
                                         op0=ALU.add)
 
@@ -249,7 +251,18 @@ def tile_kernelloglikelihood_t_kernel(tc, x, pca_weight, pca_bias, X_ref, bandwi
                                     scalar2=0.0, op0=ALU.mult, op1=ALU.add)
             zgs[k] = zg
 
+        def by_gram(k, a):
+            return a == 0 and k % 2 == 0 and 4 <= k < 30
+
+        def diag(k, a):
+            n = 2 * k + a
+            gjunk = work.tile([P, P], BF16, tag="gjunk", bufs=2, name="gjunk")
+            nc.vector.scalar_tensor_tensor(out=gjunk[:], in0=z2ps.pop((k, a))[:, 0, :], scalar=ns_ap[:, 0:1], in1=identf[:],
+                                           op0=ALU.mult, op1=ALU.mult, accum_out=nega_all[:, n:n + 1])
+
         def sq(k, a):
+            if by_gram(k, a):
+                return
             n = 2 * k + a
             sjunk = work.tile([P, 4 * P], BF16, tag="sjunk", bufs=2, name="sjunk")
             nc.scalar.activation(out=sjunk[:], in_=z2ps.pop((k, a))[:].rearrange("p t c -> p (t c)"), func=ACT.Square,
@@ -276,11 +289,15 @@ def tile_kernelloglikelihood_t_kernel(tc, x, pca_weight, pca_bias, X_ref, bandwi
             for a in range(2):
                 ztp = psum.tile([P, 4, P], F32, tag="ZT", bufs=PS_BUFS["ZT"], name="ztp")
                 for t in range(4):
-                    nc.tensor.transpose(ztp[:, t, :], zf[:, t, P * a:P * a + P], identf[:])
+                    zt = zf[:, t, P * a:P * a + P]
+                    if by_gram(k, a):
+                        nc.tensor.matmul(out=ztp[:, 0, :], lhsT=zt, rhs=zt, start=t == 0, stop=t == 3)
+                    else:
+                        nc.tensor.transpose(ztp[:, t, :], zt, identf[:])
                 z2ps[(k, a)] = ztp
 
         def nega(k):
-            nc.scalar.activation(out=nega_all[:, 2 * k - 2:2 * k + 2], in_=a_all[:, 2 * k - 2:2 * k + 2], func=ACT.Copy,
+            nc.scalar.activation(out=nega_all[:, 2 * k - 2 + by_gram(k - 1, 0):2 * k + 2], in_=a_all[:, 2 * k - 2 + by_gram(k - 1, 0):2 * k + 2], func=ACT.Copy,
                                  scale=-1.0)
 
         def stt(k):
@@ -365,6 +382,9 @@ def tile_kernelloglikelihood_t_kernel(tc, x, pca_weight, pca_bias, X_ref, bandwi
                 if valid(j - 3):
                     stt(j - 3)
                 cms(j - 4)
+            for a in range(2):
+                if valid(j - 1) and by_gram(j - 1, a):
+                    diag(j - 1, a)
             for k in xs_now:
                 q_x(k)
             if j == NPAIR:

@@ -115,29 +115,8 @@ def tile_kernelloglikelihood_t_kernel(tc, x, pca_weight, pca_bias, X_ref, bandwi
         rh = small("rh")
         rinv = small("rinv")
         n2s = small("n2s")
-        ns_ap = small("ns_ap")
         s_ap = small("s_ap")
         rsq = small("rsq")
-        t_w(0)
-        t_x(0)
-        t_w(1)
-        t_x(1, "ZT")
-        copy_out("w0", on_vector=True)
-        copy_out(0)
-        copy_out("w1")
-        nc.vector.tensor_copy(out=h32[:], in_=hb[:])
-        nc.vector.tensor_copy(out=b32[:], in_=bsb[:])
-        q_w(0)
-        nc.vector.tensor_tensor(out=hh[:], in0=h32[:], in1=h32[:], op=ALU.mult)
-        nc.vector.reciprocal(out=rinv[:], in_=h32[:])
-        q_x(0)
-        nc.vector.reciprocal(out=rh[:], in_=hh[:])
-        nc.vector.tensor_scalar(out=rsq[:], in0=rinv[:], scalar1=math.sqrt(0.5), scalar2=None, op0=ALU.mult)
-        q_w(1)
-        nc.vector.tensor_scalar(out=n2s[:], in0=rh[:], scalar1=-1.0, scalar2=None, op0=ALU.mult)
-        nc.vector.tensor_scalar(out=s_ap[:], in0=rh[:], scalar1=0.5, scalar2=None, op0=ALU.mult)
-        nc.vector.tensor_scalar(out=ns_ap[:], in0=rh[:], scalar1=-0.5, scalar2=None, op0=ALU.mult)
-
         ei = small("ei", I32)
         mi = small("mi", I32)
         ef = small("ef")
@@ -149,40 +128,52 @@ def tile_kernelloglikelihood_t_kernel(tc, x, pca_weight, pca_bias, X_ref, bandwi
         den = small("den")
         rden = small("rden")
         wq = small("wq")
-        mant = mi[:].bitcast(F32)
-        ln_steps = [
-            lambda: nc.vector.tensor_single_scalar(out=ei[:], in_=h32[:].bitcast(I32), scalar=23,
-                                                   op=ALU.logical_shift_right),
-            lambda: nc.vector.tensor_scalar(out=mi[:], in0=h32[:].bitcast(I32), scalar1=0x007FFFFF,
-                                            scalar2=0x3F800000, op0=ALU.bitwise_and, op1=ALU.bitwise_or),
-            lambda: nc.vector.tensor_copy(out=ef[:], in_=ei[:]),
-            lambda: nc.vector.tensor_single_scalar(out=gt[:], in_=mant, scalar=math.sqrt(2.0), op=ALU.is_gt),
-            lambda: nc.gpsimd.tensor_scalar(out=halve[:], in0=gt[:], scalar1=-0.5, scalar2=1.0,
-                                            op0=ALU.mult, op1=ALU.add),
-            lambda: nc.gpsimd.tensor_tensor(out=m2[:], in0=mant, in1=halve[:], op=ALU.mult),
-            lambda: nc.gpsimd.tensor_scalar(out=e3[:], in0=ef[:], scalar1=-127.0, scalar2=gt[:, 0:1],
-                                            op0=ALU.add, op1=ALU.add),
-            lambda: nc.gpsimd.tensor_scalar(out=num[:], in0=m2[:], scalar1=-1.0, scalar2=None, op0=ALU.add),
-            lambda: nc.gpsimd.tensor_scalar(out=den[:], in0=m2[:], scalar1=1.0, scalar2=None, op0=ALU.add),
-            lambda: nc.vector.reciprocal(out=rden[:], in_=den[:]),
-            lambda: nc.gpsimd.tensor_tensor(out=wq[:], in0=num[:], in1=rden[:], op=ALU.mult),
-        ]
-        coeff = small("coeff")
-
         w2 = small("w2")
         polys = [small("poly%d" % i) for i in range(8)]
         wp = small("wp")
         c1 = small("c1")
+        coeff = small("coeff")
+        mant = mi[:].bitcast(F32)
+
+        t_w(0)
+        t_x(0)
+        t_w(1)
+        t_x(1, "ZT")
+        nc.vector.tensor_copy(out=h32[:], in_=hb[:])
+        nc.vector.tensor_single_scalar(out=ei[:], in_=h32[:].bitcast(I32), scalar=23, op=ALU.logical_shift_right)
+        nc.vector.tensor_scalar(out=mi[:], in0=h32[:].bitcast(I32), scalar1=0x007FFFFF, scalar2=0x3F800000,
+                                op0=ALU.bitwise_and, op1=ALU.bitwise_or)
+        nc.vector.tensor_tensor(out=hh[:], in0=h32[:], in1=h32[:], op=ALU.mult)
+        nc.vector.reciprocal(out=rinv[:], in_=h32[:])
+        nc.vector.tensor_copy(out=ef[:], in_=ei[:])
+        nc.vector.tensor_single_scalar(out=gt[:], in_=mant, scalar=math.sqrt(2.0), op=ALU.is_gt)
+        nc.gpsimd.tensor_scalar(out=halve[:], in0=gt[:], scalar1=-0.5, scalar2=1.0, op0=ALU.mult, op1=ALU.add)
+        nc.gpsimd.tensor_tensor(out=m2[:], in0=mant, in1=halve[:], op=ALU.mult)
+        nc.gpsimd.tensor_scalar(out=e3[:], in0=ef[:], scalar1=-127.0, scalar2=gt[:, 0:1], op0=ALU.add, op1=ALU.add)
+        nc.gpsimd.tensor_scalar(out=den[:], in0=m2[:], scalar1=1.0, scalar2=None, op0=ALU.add)
+        nc.gpsimd.tensor_scalar(out=num[:], in0=m2[:], scalar1=-1.0, scalar2=None, op0=ALU.add)
+        copy_out("w0", on_vector=True)
+        copy_out(0)
+        copy_out("w1")
+        nc.vector.tensor_copy(out=b32[:], in_=bsb[:])
+        nc.vector.reciprocal(out=rh[:], in_=hh[:])
+        q_w(0)
+        nc.vector.tensor_scalar(out=rsq[:], in0=rinv[:], scalar1=math.sqrt(0.5), scalar2=None, op0=ALU.mult)
+        nc.vector.tensor_scalar(out=n2s[:], in0=rh[:], scalar1=-1.0, scalar2=None, op0=ALU.mult)
+        q_x(0)
+        nc.vector.tensor_scalar(out=s_ap[:], in0=rh[:], scalar1=0.5, scalar2=None, op0=ALU.mult)
+        q_w(1)
+        nc.vector.reciprocal(out=rden[:], in_=den[:])
+        nc.gpsimd.tensor_tensor(out=wq[:], in0=num[:], in1=rden[:], op=ALU.mult)
+        nc.gpsimd.tensor_tensor(out=w2[:], in0=wq[:], in1=wq[:], op=ALU.mult)
+        nc.gpsimd.tensor_scalar(out=polys[0][:], in0=w2[:], scalar1=1.0 / 17.0, scalar2=1.0 / 15.0,
+                                op0=ALU.mult, op1=ALU.add)
 
         def horner(i, odd):
             return lambda: nc.gpsimd.tensor_scalar(out=polys[i][:], in0=polys[i - 1][:], scalar1=w2[:, 0:1],
                                                    scalar2=1.0 / odd, op0=ALU.mult, op1=ALU.add)
 
-        series_steps = [
-            lambda: nc.gpsimd.tensor_tensor(out=w2[:], in0=wq[:], in1=wq[:], op=ALU.mult),
-            lambda: nc.gpsimd.tensor_scalar(out=polys[0][:], in0=w2[:], scalar1=1.0 / 17.0, scalar2=1.0 / 15.0,
-                                            op0=ALU.mult, op1=ALU.add),
-        ] + [horner(i + 1, odd) for i, odd in enumerate((13, 11, 9, 7, 5, 3, 1))] + [
+        series_steps = [horner(i + 1, odd) for i, odd in enumerate((13, 11, 9, 7, 5, 3, 1))] + [
             lambda: nc.gpsimd.tensor_tensor(out=wp[:], in0=polys[7][:], in1=wq[:], op=ALU.mult),
             lambda: nc.gpsimd.tensor_scalar(out=c1[:], in0=e3[:], scalar1=-DC * math.log(2.0),
                                             scalar2=-math.log(NREF) - 0.5 * DC * math.log(2.0 * math.pi),
@@ -252,13 +243,13 @@ def tile_kernelloglikelihood_t_kernel(tc, x, pca_weight, pca_bias, X_ref, bandwi
             zgs[k] = zg
 
         def by_gram(k, a):
-            return a == 0 and k % 2 == 0 and 4 <= k < 30
+            return a == 1 and k % 2 == 0 and 4 <= k < 30
 
         def diag(k, a):
             n = 2 * k + a
             gjunk = work.tile([P, P], BF16, tag="gjunk", bufs=2, name="gjunk")
-            nc.vector.scalar_tensor_tensor(out=gjunk[:], in0=z2ps.pop((k, a))[:, 0, :], scalar=ns_ap[:, 0:1], in1=identf[:],
-                                           op0=ALU.mult, op1=ALU.mult, accum_out=nega_all[:, n:n + 1])
+            nc.vector.scalar_tensor_tensor(out=gjunk[:], in0=z2ps.pop((k, a))[:, 0, :], scalar=s_ap[:, 0:1], in1=identf[:],
+                                           op0=ALU.mult, op1=ALU.mult, accum_out=a_all[:, n:n + 1])
 
         def sq(k, a):
             if by_gram(k, a):
@@ -297,7 +288,7 @@ def tile_kernelloglikelihood_t_kernel(tc, x, pca_weight, pca_bias, X_ref, bandwi
                 z2ps[(k, a)] = ztp
 
         def nega(k):
-            nc.scalar.activation(out=nega_all[:, 2 * k - 2 + by_gram(k - 1, 0):2 * k + 2], in_=a_all[:, 2 * k - 2 + by_gram(k - 1, 0):2 * k + 2], func=ACT.Copy,
+            nc.scalar.activation(out=nega_all[:, 2 * k - 2:2 * k + 2], in_=a_all[:, 2 * k - 2:2 * k + 2], func=ACT.Copy,
                                  scale=-1.0)
 
         def stt(k):
@@ -320,8 +311,7 @@ def tile_kernelloglikelihood_t_kernel(tc, x, pca_weight, pca_bias, X_ref, bandwi
             nc.scalar.activation(out=ejunk[:], in_=ucls[k][:, a, :], func=ACT.Exp, bias=mn_all[:, n:n + 1], scale=-1.0,
                                  accum_out=sum_all[:, n:n + 1])
 
-        LN0 = 3
-        SER0 = LN0 + len(ln_steps) + 1
+        SER0 = 3
 
         def x_steps(j):
             first = {1: 3, 2: 5}.get(j, j + 4)
@@ -364,7 +354,7 @@ def tile_kernelloglikelihood_t_kernel(tc, x, pca_weight, pca_bias, X_ref, bandwi
                 z2(j - 1)
             if xs_now:
                 x_step(xs_now[0])
-            if j == 1:
+            if j == 2:
                 r2t = psum.tile([P, 2, P], F32, tag="G", bufs=PS_BUFS["G"], name="r2t")
                 for jt in range(2):
                     nc.tensor.matmul(out=r2t[:, jt, :], lhsT=r2[:, jt:jt + 1].to_broadcast([P, P]), rhs=identf[:],
@@ -382,11 +372,11 @@ def tile_kernelloglikelihood_t_kernel(tc, x, pca_weight, pca_bias, X_ref, bandwi
                 if valid(j - 3):
                     stt(j - 3)
                 cms(j - 4)
+            for k in xs_now:
+                q_x(k)
             for a in range(2):
                 if valid(j - 1) and by_gram(j - 1, a):
                     diag(j - 1, a)
-            for k in xs_now:
-                q_x(k)
             if j == NPAIR:
                 stt(j - 3)
                 cms(j - 4)
@@ -404,13 +394,11 @@ def tile_kernelloglikelihood_t_kernel(tc, x, pca_weight, pca_bias, X_ref, bandwi
                 cms(j - 2)
             if j == 1:
                 quantise("r", rc[:], rsc[:])
-            if LN0 <= j < LN0 + len(ln_steps):
-                ln_steps[j - LN0]()
             if SER0 <= j < SER0 + len(series_steps):
                 series_steps[j - SER0]()
             if valid(j):
                 cast(j)
-            if j == 1:
+            if j == 2:
                 nc.scalar.activation(out=csb[:], in_=r2t[:].rearrange("p a j -> p (a j)"), func=ACT.Copy,
                                      scale=s_ap[:, 0:1])
             if valid(j - 2) and j % 2 == 1 and j < NPAIR:

@@ -34,10 +34,12 @@ def tile_kernelloglikelihood_t_kernel(tc, x, pca_weight, pca_bias, X_ref, bandwi
         work = ctx.enter_context(tc.tile_pool(name="work", bufs=3))
         psum = ctx.enter_context(tc.psum_pool(name="psum", bufs=2))
 
-        hb = const.tile([P, 1], BF16)
-        nc.scalar.dma_start(out=hb[:], in_=bandwidth.partition_broadcast(P))
+        hcol = const.tile([P, 2], BF16)
+        nc.gpsimd.memset(hcol[:], 0.0)
+        nc.scalar.dma_start(out=hcol[0:1, 0:1], in_=bandwidth.rearrange("(a b) -> a b", b=1))
+        ones = const.tile([P, P], BF16)
+        nc.gpsimd.memset(ones[:], 1.0)
         bsb = const.tile([P, 4], BF16)
-        nc.scalar.dma_start(out=bsb[:], in_=pca_bias.rearrange("(p t) -> p t", t=4))
         wsb = const.tile([P, 4, D], BF16)
         wv = pca_weight.rearrange("(p t) k -> p t k", t=4)
         nc.sync.dma_start(out=wsb[:, 0:2, :], in_=wv[:, 0:2, :])
@@ -54,6 +56,7 @@ def tile_kernelloglikelihood_t_kernel(tc, x, pca_weight, pca_bias, X_ref, bandwi
             n0 += cn
             if ci == 0:
                 nc.sync.dma_start(out=wsb[:, 2:4, :], in_=wv[:, 2:4, :])
+                nc.sync.dma_start(out=bsb[:], in_=pca_bias.rearrange("(p t) -> p t", t=4))
             if ci == 2:
                 nc.sync.dma_start(out=rsb[:], in_=X_ref.rearrange("(p j) c -> p j c", j=2))
 
@@ -75,7 +78,7 @@ def tile_kernelloglikelihood_t_kernel(tc, x, pca_weight, pca_bias, X_ref, bandwi
 
         def copy_out(key, on_vector=False):
             tp = tps.pop(key)
-            grouped = work.tile([P, 2 * P * 4], BF16, tag="grouped", bufs=3, align_bytes=64, name="grouped")
+            grouped = work.tile([P, 2 * P * 4], BF16, tag="grouped", bufs=4, align_bytes=64, name="grouped")
             dst = grouped[:].bitcast(F32).rearrange("p (a i u) -> p a i u", a=2, u=2)
             src = tp[:].rearrange("p a u i -> p a i u")
             if on_vector:
@@ -117,6 +120,21 @@ def tile_kernelloglikelihood_t_kernel(tc, x, pca_weight, pca_bias, X_ref, bandwi
         n2s = small("n2s")
         s_ap = small("s_ap")
         rsq = small("rsq")
+        t_w(0)
+        t_x(0)
+        t_w(1)
+        t_x(1, "ZT")
+        hps = psum.tile([P, 1], F32, tag="G", bufs=PS_BUFS["G"], name="hps")
+        nc.tensor.matmul(out=hps[:], lhsT=ones[:], rhs=hcol[:, 0:1], start=True, stop=True)
+        copy_out("w0", on_vector=True)
+        copy_out(0)
+        copy_out("w1")
+        q_w(0)
+        q_x(0)
+        q_w(1)
+        nc.vector.tensor_copy(out=b32[:], in_=bsb[:])
+        nc.vector.tensor_copy(out=h32[:], in_=hps[:])
+
         ei = small("ei", I32)
         mi = small("mi", I32)
         ef = small("ef")
@@ -128,52 +146,40 @@ def tile_kernelloglikelihood_t_kernel(tc, x, pca_weight, pca_bias, X_ref, bandwi
         den = small("den")
         rden = small("rden")
         wq = small("wq")
+        mant = mi[:].bitcast(F32)
+        ln_steps = [
+            lambda: nc.vector.tensor_single_scalar(out=ei[:], in_=h32[:].bitcast(I32), scalar=23,
+                                                   op=ALU.logical_shift_right),
+            lambda: nc.vector.tensor_scalar(out=mi[:], in0=h32[:].bitcast(I32), scalar1=0x007FFFFF,
+                                            scalar2=0x3F800000, op0=ALU.bitwise_and, op1=ALU.bitwise_or),
+            lambda: nc.vector.tensor_copy(out=ef[:], in_=ei[:]),
+            lambda: nc.vector.tensor_single_scalar(out=gt[:], in_=mant, scalar=math.sqrt(2.0), op=ALU.is_gt),
+            lambda: nc.gpsimd.tensor_scalar(out=halve[:], in0=gt[:], scalar1=-0.5, scalar2=1.0,
+                                            op0=ALU.mult, op1=ALU.add),
+            lambda: nc.gpsimd.tensor_tensor(out=m2[:], in0=mant, in1=halve[:], op=ALU.mult),
+            lambda: nc.gpsimd.tensor_scalar(out=e3[:], in0=ef[:], scalar1=-127.0, scalar2=gt[:, 0:1],
+                                            op0=ALU.add, op1=ALU.add),
+            lambda: nc.gpsimd.tensor_scalar(out=num[:], in0=m2[:], scalar1=-1.0, scalar2=None, op0=ALU.add),
+            lambda: nc.gpsimd.tensor_scalar(out=den[:], in0=m2[:], scalar1=1.0, scalar2=None, op0=ALU.add),
+            lambda: nc.vector.reciprocal(out=rden[:], in_=den[:]),
+            lambda: nc.gpsimd.tensor_tensor(out=wq[:], in0=num[:], in1=rden[:], op=ALU.mult),
+        ]
+        coeff = small("coeff")
+
         w2 = small("w2")
         polys = [small("poly%d" % i) for i in range(8)]
         wp = small("wp")
         c1 = small("c1")
-        coeff = small("coeff")
-        mant = mi[:].bitcast(F32)
-
-        t_w(0)
-        t_x(0)
-        t_w(1)
-        t_x(1, "ZT")
-        nc.vector.tensor_copy(out=h32[:], in_=hb[:])
-        nc.vector.tensor_single_scalar(out=ei[:], in_=h32[:].bitcast(I32), scalar=23, op=ALU.logical_shift_right)
-        nc.vector.tensor_scalar(out=mi[:], in0=h32[:].bitcast(I32), scalar1=0x007FFFFF, scalar2=0x3F800000,
-                                op0=ALU.bitwise_and, op1=ALU.bitwise_or)
-        nc.vector.tensor_tensor(out=hh[:], in0=h32[:], in1=h32[:], op=ALU.mult)
-        nc.vector.reciprocal(out=rinv[:], in_=h32[:])
-        nc.vector.tensor_copy(out=ef[:], in_=ei[:])
-        nc.vector.tensor_single_scalar(out=gt[:], in_=mant, scalar=math.sqrt(2.0), op=ALU.is_gt)
-        nc.gpsimd.tensor_scalar(out=halve[:], in0=gt[:], scalar1=-0.5, scalar2=1.0, op0=ALU.mult, op1=ALU.add)
-        nc.gpsimd.tensor_tensor(out=m2[:], in0=mant, in1=halve[:], op=ALU.mult)
-        nc.gpsimd.tensor_scalar(out=e3[:], in0=ef[:], scalar1=-127.0, scalar2=gt[:, 0:1], op0=ALU.add, op1=ALU.add)
-        nc.gpsimd.tensor_scalar(out=den[:], in0=m2[:], scalar1=1.0, scalar2=None, op0=ALU.add)
-        nc.gpsimd.tensor_scalar(out=num[:], in0=m2[:], scalar1=-1.0, scalar2=None, op0=ALU.add)
-        copy_out("w0", on_vector=True)
-        copy_out(0)
-        copy_out("w1")
-        nc.vector.tensor_copy(out=b32[:], in_=bsb[:])
-        nc.vector.reciprocal(out=rh[:], in_=hh[:])
-        q_w(0)
-        nc.vector.tensor_scalar(out=rsq[:], in0=rinv[:], scalar1=math.sqrt(0.5), scalar2=None, op0=ALU.mult)
-        nc.vector.tensor_scalar(out=n2s[:], in0=rh[:], scalar1=-1.0, scalar2=None, op0=ALU.mult)
-        q_x(0)
-        nc.vector.tensor_scalar(out=s_ap[:], in0=rh[:], scalar1=0.5, scalar2=None, op0=ALU.mult)
-        q_w(1)
-        nc.vector.reciprocal(out=rden[:], in_=den[:])
-        nc.gpsimd.tensor_tensor(out=wq[:], in0=num[:], in1=rden[:], op=ALU.mult)
-        nc.gpsimd.tensor_tensor(out=w2[:], in0=wq[:], in1=wq[:], op=ALU.mult)
-        nc.gpsimd.tensor_scalar(out=polys[0][:], in0=w2[:], scalar1=1.0 / 17.0, scalar2=1.0 / 15.0,
-                                op0=ALU.mult, op1=ALU.add)
 
         def horner(i, odd):
             return lambda: nc.gpsimd.tensor_scalar(out=polys[i][:], in0=polys[i - 1][:], scalar1=w2[:, 0:1],
                                                    scalar2=1.0 / odd, op0=ALU.mult, op1=ALU.add)
 
-        series_steps = [horner(i + 1, odd) for i, odd in enumerate((13, 11, 9, 7, 5, 3, 1))] + [
+        series_steps = [
+            lambda: nc.gpsimd.tensor_tensor(out=w2[:], in0=wq[:], in1=wq[:], op=ALU.mult),
+            lambda: nc.gpsimd.tensor_scalar(out=polys[0][:], in0=w2[:], scalar1=1.0 / 17.0, scalar2=1.0 / 15.0,
+                                            op0=ALU.mult, op1=ALU.add),
+        ] + [horner(i + 1, odd) for i, odd in enumerate((13, 11, 9, 7, 5, 3, 1))] + [
             lambda: nc.gpsimd.tensor_tensor(out=wp[:], in0=polys[7][:], in1=wq[:], op=ALU.mult),
             lambda: nc.gpsimd.tensor_scalar(out=c1[:], in0=e3[:], scalar1=-DC * math.log(2.0),
                                             scalar2=-math.log(NREF) - 0.5 * DC * math.log(2.0 * math.pi),
@@ -247,7 +253,7 @@ def tile_kernelloglikelihood_t_kernel(tc, x, pca_weight, pca_bias, X_ref, bandwi
 
         def diag(k, a):
             n = 2 * k + a
-            gjunk = work.tile([P, P], BF16, tag="gjunk", bufs=2, name="gjunk")
+            gjunk = work.tile([P, P], BF16, tag="gjunk", bufs=4, name="gjunk")
             nc.vector.scalar_tensor_tensor(out=gjunk[:], in0=z2ps.pop((k, a))[:, 0, :], scalar=s_ap[:, 0:1], in1=identf[:],
                                            op0=ALU.mult, op1=ALU.mult, accum_out=a_all[:, n:n + 1])
 
@@ -255,7 +261,7 @@ def tile_kernelloglikelihood_t_kernel(tc, x, pca_weight, pca_bias, X_ref, bandwi
             if by_gram(k, a):
                 return
             n = 2 * k + a
-            sjunk = work.tile([P, 4 * P], BF16, tag="sjunk", bufs=2, name="sjunk")
+            sjunk = work.tile([P, 4 * P], BF16, tag="sjunk", bufs=8, name="sjunk")
             nc.scalar.activation(out=sjunk[:], in_=z2ps.pop((k, a))[:].rearrange("p t c -> p (t c)"), func=ACT.Square,
                                  scale=rsq[:, 0:1], accum_out=a_all[:, n:n + 1])
 
@@ -292,7 +298,7 @@ def tile_kernelloglikelihood_t_kernel(tc, x, pca_weight, pca_bias, X_ref, bandwi
                                  scale=-1.0)
 
         def stt(k):
-            u = work.tile([P, 2, NREF], F32, tag="u", bufs=2, name="u")
+            u = work.tile([P, 2, NREF], F32, tag="u", bufs=4, name="u")
             nc.vector.scalar_tensor_tensor(out=u[:], in0=gps.pop(k)[:], scalar=n2s[:, 0:1],
                                            in1=csb[:].unsqueeze(1).to_broadcast([P, 2, NREF]),
                                            op0=ALU.mult, op1=ALU.add)
@@ -300,18 +306,19 @@ def tile_kernelloglikelihood_t_kernel(tc, x, pca_weight, pca_bias, X_ref, bandwi
 
         def cm(k, a):
             if a == 0:
-                ucls[k] = work.tile([P, 2, NREF], F32, tag="ucl", bufs=4, name="ucl")
+                ucls[k] = work.tile([P, 2, NREF], F32, tag="ucl", bufs=6, name="ucl")
             n = 2 * k + a
             nc.vector.tensor_scalar(out=ucls[k][:, a, :], in0=us[k][:, a, :], scalar1=nega_all[:, n:n + 1], scalar2=None,
                                     op0=ALU.max, op1=ALU.min, accum_out=mn_all[:, n:n + 1])
 
         def ex(k, a):
             n = 2 * k + a
-            ejunk = work.tile([P, NREF], BF16, tag="ejunk", bufs=2, name="ejunk")
+            ejunk = work.tile([P, NREF], BF16, tag="ejunk", bufs=8, name="ejunk")
             nc.scalar.activation(out=ejunk[:], in_=ucls[k][:, a, :], func=ACT.Exp, bias=mn_all[:, n:n + 1], scale=-1.0,
                                  accum_out=sum_all[:, n:n + 1])
 
-        SER0 = 3
+        LN0 = 3
+        SER0 = LN0 + len(ln_steps) + 1
 
         def x_steps(j):
             first = {1: 3, 2: 5}.get(j, j + 4)
@@ -334,14 +341,20 @@ def tile_kernelloglikelihood_t_kernel(tc, x, pca_weight, pca_bias, X_ref, bandwi
         q_x(1)
         r_square(0)
         s1(1, 0)
+        nc.vector.tensor_tensor(out=hh[:], in0=h32[:], in1=h32[:], op=ALU.mult)
+        nc.vector.reciprocal(out=rinv[:], in_=h32[:])
         plane(0)
         ev(0, 0)
         copy_out(2)
         s1(1, 1)
+        nc.vector.reciprocal(out=rh[:], in_=hh[:])
+        nc.vector.tensor_scalar(out=rsq[:], in0=rinv[:], scalar1=math.sqrt(0.5), scalar2=None, op0=ALU.mult)
         ev(0, 1)
         t_x(3)
         q_x(2)
         cast(0)
+        nc.vector.tensor_scalar(out=n2s[:], in0=rh[:], scalar1=-1.0, scalar2=None, op0=ALU.mult)
+        nc.vector.tensor_scalar(out=s_ap[:], in0=rh[:], scalar1=0.5, scalar2=None, op0=ALU.mult)
         transposes("r", [r32[:, i // 2, (i % 2):256:2] for i in range(4)], "G")
         t_x(4, "G")
         r_square(1)
@@ -394,6 +407,8 @@ def tile_kernelloglikelihood_t_kernel(tc, x, pca_weight, pca_bias, X_ref, bandwi
                 cms(j - 2)
             if j == 1:
                 quantise("r", rc[:], rsc[:])
+            if LN0 <= j < LN0 + len(ln_steps):
+                ln_steps[j - LN0]()
             if SER0 <= j < SER0 + len(series_steps):
                 series_steps[j - SER0]()
             if valid(j):

@@ -249,7 +249,7 @@ def tile_kernelloglikelihood_t_kernel(tc, x, pca_weight, pca_bias, X_ref, bandwi
             zgs[k] = zg
 
         def by_gram(k, a):
-            return a == 1 and k % 2 == 0 and 4 <= k < 30
+            return a == 1 and k % 2 == 0 and 4 <= k
 
         def diag(k, a):
             n = 2 * k + a
@@ -325,7 +325,7 @@ def tile_kernelloglikelihood_t_kernel(tc, x, pca_weight, pca_bias, X_ref, bandwi
             return [k for k in ([first, first + 1] if j < 3 else [first]) if k < NPAIR]
 
         def x_step(k):
-            copy_out(k, on_vector=k in (3, 5))
+            copy_out(k, on_vector=k == 3)
             if k + 1 < NPAIR and k + 1 != 4:
                 t_x(k + 1)
 
@@ -385,11 +385,11 @@ def tile_kernelloglikelihood_t_kernel(tc, x, pca_weight, pca_bias, X_ref, bandwi
                 if valid(j - 3):
                     stt(j - 3)
                 cms(j - 4)
-            for k in xs_now:
-                q_x(k)
             for a in range(2):
                 if valid(j - 1) and by_gram(j - 1, a):
                     diag(j - 1, a)
+            for k in xs_now:
+                q_x(k)
             if j == NPAIR:
                 stt(j - 3)
                 cms(j - 4)

@@ -244,8 +244,9 @@ def tile_kernelloglikelihood_t_kernel(tc, x, pca_weight, pca_bias, X_ref, bandwi
 
         def cast(k):
             zg = work.tile([P, 2, P, 4], BF16, tag="zg", bufs=1, align_bytes=64, name="zg")
-            nc.gpsimd.tensor_scalar(out=zg[:], in0=zfs[k][:].rearrange("p t (a i) -> p a i t", a=2), scalar1=1.0,
-                                    scalar2=0.0, op0=ALU.mult, op1=ALU.add)
+            nc.gpsimd.tensor_scalar(out=zg[:].rearrange("p a (c i) t -> p (a c) t i", i=4),
+                                    in0=zfs[k][:].rearrange("p t (c i) -> p c t i", i=4), scalar1=1.0, scalar2=0.0,
+                                    op0=ALU.mult, op1=ALU.add)
             zgs[k] = zg
 
         def by_gram(k, a):

@@ -227,7 +227,7 @@ def tile_kernelloglikelihood_t_kernel(tc, x, pca_weight, pca_bias, X_ref, bandwi
 
         def plane(k):
             zfs[k] = work.tile([P, 4, 2 * P], F32, tag="zf", bufs=3, name="zf")
-            if k < 5:
+            if k < 4:
                 return
             for t in ((2, 3) if k >= 25 or k % 4 != 2 else (3,)):
                 nc.scalar.activation(out=zfs[k][:, t, :], in_=zps[(k, 1)][:, t - 2, :], func=ACT.Identity,
@@ -235,7 +235,7 @@ def tile_kernelloglikelihood_t_kernel(tc, x, pca_weight, pca_bias, X_ref, bandwi
 
         def ev(k, h):
             zp = zps.pop((k, h))
-            if h == 0 or k < 5:
+            if h == 0 or k < 4:
                 nc.vector.tensor_tensor(out=zfs[k][:, 2 * h:2 * h + 2, :], in0=zp[:],
                                         in1=b32[:, 2 * h:2 * h + 2].unsqueeze(2).to_broadcast([P, 2, 2 * P]), op=ALU.add)
             elif not (k >= 25 or k % 4 != 2):
@@ -295,8 +295,8 @@ def tile_kernelloglikelihood_t_kernel(tc, x, pca_weight, pca_bias, X_ref, bandwi
                 z2ps[(k, a)] = ztp
 
         def nega(k):
-            nc.scalar.activation(out=nega_all[:, 2 * k - 2:2 * k + 2], in_=a_all[:, 2 * k - 2:2 * k + 2], func=ACT.Copy,
-                                 scale=-1.0)
+            nc.gpsimd.tensor_scalar(out=nega_all[:, 2 * k - 2:2 * k + 2], in0=a_all[:, 2 * k - 2:2 * k + 2],
+                                    scalar1=-1.0, scalar2=0.0, op0=ALU.mult, op1=ALU.add)
 
         def stt(k):
             u = work.tile([P, 2, NREF], F32, tag="u", bufs=4, name="u")
@@ -319,7 +319,7 @@ def tile_kernelloglikelihood_t_kernel(tc, x, pca_weight, pca_bias, X_ref, bandwi
                                  accum_out=sum_all[:, n:n + 1])
 
         LN0 = 3
-        SER0 = LN0 + len(ln_steps) + 1
+        SER0 = LN0 + len(ln_steps) - 3
 
         def x_steps(j):
             first = {1: 3, 2: 5}.get(j, j + 4)
@@ -390,6 +390,9 @@ def tile_kernelloglikelihood_t_kernel(tc, x, pca_weight, pca_bias, X_ref, bandwi
                 if valid(j - 1) and by_gram(j - 1, a):
                     diag(j - 1, a)
             for k in xs_now:
+                if j == 2 and k == xs_now[-1]:
+                    for step in ln_steps[:4]:
+                        step()
                 q_x(k)
             if j == NPAIR:
                 stt(j - 3)
@@ -408,17 +411,17 @@ def tile_kernelloglikelihood_t_kernel(tc, x, pca_weight, pca_bias, X_ref, bandwi
                 cms(j - 2)
             if j == 1:
                 quantise("r", rc[:], rsc[:])
-            if LN0 <= j < LN0 + len(ln_steps):
-                ln_steps[j - LN0]()
+            if LN0 <= j < LN0 + len(ln_steps) - 4:
+                ln_steps[j - LN0 + 4]()
             if SER0 <= j < SER0 + len(series_steps):
                 series_steps[j - SER0]()
+            if valid(j - 2) and j % 2 == 1 and j < NPAIR:
+                nega(j - 2)
             if valid(j):
                 cast(j)
             if j == 2:
                 nc.scalar.activation(out=csb[:], in_=r2t[:].rearrange("p a j -> p (a j)"), func=ACT.Copy,
                                      scale=s_ap[:, 0:1])
-            if valid(j - 2) and j % 2 == 1 and j < NPAIR:
-                nega(j - 2)
             if valid(j - 5):
                 ex(j - 5, 0)
                 ex(j - 5, 1)

import math
from contextlib import ExitStack

import concourse.mybir as mybir
from concourse.masks import make_identity

FLOPS = 2 * 8192 * 512 * 512 + 2 * 8192 * 512 * 256

F32 = mybir.dt.float32
BF16 = mybir.dt.bfloat16
U32 = mybir.dt.uint32
U8 = mybir.dt.uint8
I32 = mybir.dt.int32
FP8X4 = mybir.dt.float8_e4m3fn_x4
ALU = mybir.AluOpType
ACT = mybir.ActivationFunctionType

P = 128
B = 8192
D = 512
DC = 512
NREF = 256
NT = B // P
NPAIR = NT // 2
CHUNKS = (2, 2, 4, 4, 4, 8, 8, 8, 8, 8, 8)
PS_BUFS = {"xT": 1, "Z": 3, "G": 2, "ZT": 2}


def tile_kernelloglikelihood_t_kernel(tc, x, pca_weight, pca_bias, X_ref, bandwidth, out):
    nc = tc.nc
    with ExitStack() as ctx:
        ctx.enter_context(tc.manual_schedule())
        const = ctx.enter_context(tc.tile_pool(name="const", bufs=1))
        work = ctx.enter_context(tc.tile_pool(name="work", bufs=3))
        psum = ctx.enter_context(tc.psum_pool(name="psum", bufs=2))

        hcol = const.tile([P, 2], BF16)
        nc.gpsimd.memset(hcol[:], 0.0)
        nc.scalar.dma_start(out=hcol[0:1, 0:1], in_=bandwidth.rearrange("(a b) -> a b", b=1))
        ones = const.tile([P, P], BF16)
        nc.gpsimd.memset(ones[:], 1.0)
        bsb = const.tile([P, 4], BF16)
        wsb = const.tile([P, 4, D], BF16)
        wv = pca_weight.rearrange("(p t) k -> p t k", t=4)
        nc.sync.dma_start(out=wsb[:, 0:2, :], in_=wv[:, 0:2, :])
        xv = x.rearrange("(p n) k -> p n k", n=NT)
        xw = []
        n0 = 0
        rsb = const.tile([P, 2, DC], BF16)
        for ci, cn in enumerate(CHUNKS):
            xt = const.tile([P, cn, D], BF16, name="xchunk%d" % ci)
            nc.sync.dma_start(out=xt[:], in_=xv[:, n0:n0 + cn, :])
            xt32 = xt[:].bitcast(F32)
            for k in range(cn):
                xw.append(xt32[:, k, :])
            n0 += cn
            if ci == 0:
                nc.sync.dma_start(out=wsb[:, 2:4, :], in_=wv[:, 2:4, :])
                nc.sync.dma_start(out=bsb[:], in_=pca_bias.rearrange("(p t) -> p t", t=4))
            if ci == 2:
                nc.sync.dma_start(out=rsb[:], in_=X_ref.rearrange("(p j) c -> p j c", j=2))

        identf = const.tile([P, P], F32)
        make_identity(nc, identf[:])

        def small(name, dt=F32, w=1):
            return const.tile([P, w], dt, name=name)

        tps = {}
        groupeds = {}

        def transposes(key, srcs, tag):
            tp = psum.tile([P, 2, 2, P], F32, tag=tag, bufs=PS_BUFS[tag], name="tp")
            for a in range(2):
                for u in range(2):
                    nc.tensor.transpose(tp[:, a, u, :], srcs[2 * a + u], identf[:])
            tps[key] = tp

        def copy_out(key, on_vector=False):
            tp = tps.pop(key)
            grouped = work.tile([P, 2 * P * 4], BF16, tag="grouped", bufs=4, align_bytes=64, name="grouped")
            dst = grouped[:].bitcast(F32).rearrange("p (a i u) -> p a i u", a=2, u=2)
            src = tp[:].rearrange("p a u i -> p a i u")
            if on_vector:
                nc.vector.tensor_copy(out=dst, in_=src)
            else:
                nc.scalar.copy(out=dst, in_=src)
            groupeds[key] = grouped

        def quantise(key, codes, scales):
            grouped = groupeds.pop(key)
            nc.vector.quantize_mx(out=codes.bitcast(FP8X4), scales=scales, in_=grouped[:])

        wc = const.tile([P, 4 * P], U32, align_bytes=64)
        wsc = const.tile([P, 4 * P], U8, align_bytes=64)
        w32 = wsb[:].bitcast(F32)

        def t_w(a):
            transposes("w%d" % a, [w32[:, 2 * a + (i // 2), P * (i % 2):P * (i % 2) + P] for i in range(4)], "Z")

        def q_w(a):
            quantise("w%d" % a, wc[:, 256 * a:256 * a + 256], wsc[:, 256 * a:256 * a + 256])

        xcodes = {}

        def t_x(k, tag="xT"):
            transposes(k, [xw[2 * k + (i // 2)][:, P * (i % 2):P * (i % 2) + P] for i in range(4)], tag)

        def q_x(k):
            xc = work.tile([P, 2 * P], U32, tag="xc", bufs=8, align_bytes=64, name="xc")
            xs = work.tile([P, 2 * P], U8, tag="xs", bufs=8, align_bytes=64, name="xs")
            quantise(k, xc[:], xs[:])
            xcodes[k] = (xc, xs)

        h32 = small("h32")
        b32 = small("b32", w=4)
        hh = small("hh")
        rh = small("rh")
        rinv = small("rinv")
        n2s = small("n2s")
        s_ap = small("s_ap")
        rsq = small("rsq")
        t_w(0)
        t_x(0)
        t_w(1)
        t_x(1, "ZT")
        hps = psum.tile([P, 1], F32, tag="G", bufs=PS_BUFS["G"], name="hps")
        nc.tensor.matmul(out=hps[:], lhsT=ones[:], rhs=hcol[:, 0:1], start=True, stop=True)
        copy_out("w0", on_vector=True)
        copy_out(0)
        copy_out("w1")
        q_w(0)
        q_x(0)
        q_w(1)
        nc.vector.tensor_copy(out=b32[:], in_=bsb[:])
        nc.vector.tensor_copy(out=h32[:], in_=hps[:])

        ei = small("ei", I32)
        mi = small("mi", I32)
        ef = small("ef")
        gt = small("gt")
        halve = small("halve")
        m2 = small("m2")
        e3 = small("e3")
        num = small("num")
        den = small("den")
        rden = small("rden")
        wq = small("wq")
        mant = mi[:].bitcast(F32)
        ln_steps = [
            lambda: nc.vector.tensor_single_scalar(out=ei[:], in_=h32[:].bitcast(I32), scalar=23,
                                                   op=ALU.logical_shift_right),
            lambda: nc.vector.tensor_scalar(out=mi[:], in0=h32[:].bitcast(I32), scalar1=0x007FFFFF,
                                            scalar2=0x3F800000, op0=ALU.bitwise_and, op1=ALU.bitwise_or),
            lambda: nc.vector.tensor_copy(out=ef[:], in_=ei[:]),
            lambda: nc.vector.tensor_single_scalar(out=gt[:], in_=mant, scalar=math.sqrt(2.0), op=ALU.is_gt),
            lambda: nc.gpsimd.tensor_scalar(out=halve[:], in0=gt[:], scalar1=-0.5, scalar2=1.0,
                                            op0=ALU.mult, op1=ALU.add),
            lambda: nc.gpsimd.tensor_tensor(out=m2[:], in0=mant, in1=halve[:], op=ALU.mult),
            lambda: nc.gpsimd.tensor_scalar(out=e3[:], in0=ef[:], scalar1=-127.0, scalar2=gt[:, 0:1],
                                            op0=ALU.add, op1=ALU.add),
            lambda: nc.gpsimd.tensor_scalar(out=num[:], in0=m2[:], scalar1=-1.0, scalar2=None, op0=ALU.add),
            lambda: nc.gpsimd.tensor_scalar(out=den[:], in0=m2[:], scalar1=1.0, scalar2=None, op0=ALU.add),
            lambda: nc.vector.reciprocal(out=rden[:], in_=den[:]),
            lambda: nc.gpsimd.tensor_tensor(out=wq[:], in0=num[:], in1=rden[:], op=ALU.mult),
        ]
        coeff = small("coeff")

        w2 = small("w2")
        polys = [small("poly%d" % i) for i in range(8)]
        wp = small("wp")
        c1 = small("c1")

        def horner(i, odd):
            return lambda: nc.gpsimd.tensor_scalar(out=polys[i][:], in0=polys[i - 1][:], scalar1=w2[:, 0:1],
                                                   scalar2=1.0 / odd, op0=ALU.mult, op1=ALU.add)

        series_steps = [
            lambda: nc.gpsimd.tensor_tensor(out=w2[:], in0=wq[:], in1=wq[:], op=ALU.mult),
            lambda: nc.gpsimd.tensor_scalar(out=polys[0][:], in0=w2[:], scalar1=1.0 / 17.0, scalar2=1.0 / 15.0,
                                            op0=ALU.mult, op1=ALU.add),
        ] + [horner(i + 1, odd) for i, odd in enumerate((13, 11, 9, 7, 5, 3, 1))] + [
            lambda: nc.gpsimd.tensor_tensor(out=wp[:], in0=polys[7][:], in1=wq[:], op=ALU.mult),
            lambda: nc.gpsimd.tensor_scalar(out=c1[:], in0=e3[:], scalar1=-DC * math.log(2.0),
                                            scalar2=-math.log(NREF) - 0.5 * DC * math.log(2.0 * math.pi),
                                            op0=ALU.mult, op1=ALU.add),
            lambda: nc.gpsimd.tensor_scalar(out=coeff[:], in0=wp[:], scalar1=-2.0 * DC, scalar2=c1[:, 0:1],
                                            op0=ALU.mult, op1=ALU.add),
        ]

        rc = const.tile([P, NREF], U32, align_bytes=64)
        rsc = const.tile([P, NREF], U8, align_bytes=64)
        r32 = rsb[:].bitcast(F32)
        r2 = small("r2", w=2)
        csb = const.tile([P, NREF], F32)

        def r_square(jt):
            rjunk = work.tile([P, DC], BF16, tag="rjunk", bufs=2, name="rjunk")
            nc.scalar.activation(out=rjunk[:], in_=rsb[:, jt, :], func=ACT.Square, accum_out=r2[:, jt:jt + 1])

        mn_all = const.tile([P, NT], F32)
        sum_all = const.tile([P, NT], F32)
        nega_all = const.tile([P, NT], F32)
        a_all = const.tile([P, NT], F32)

        zps = {}
        zfs = {}
        zgs = {}
        zcodes = {}
        z2ps = {}
        gps = {}
        us = {}
        ucls = {}

        def valid(k):
            return 0 <= k < NPAIR

        def s1(k, h):
            xc, xs = xcodes[k]
            zp = psum.tile([P, 2, 2 * P], F32, tag="Z", bufs=PS_BUFS["Z"], name="zp")
            for tt in range(2):
                t = 2 * h + tt
                nc.tensor.matmul_mx(out=zp[:, tt, :],
                                    lhsT=wc[:, P * t:P * t + P].bitcast(FP8X4), lhsT_scale=wsc[:, P * t:P * t + P],
                                    rhs=xc[:].bitcast(FP8X4), rhs_scale=xs[:], start=True, stop=True)
            zps[(k, h)] = zp

        def plane(k):
            zfs[k] = work.tile([P, 4, 2 * P], F32, tag="zf", bufs=3, name="zf")
            if k < 4:
                return
            for t in ((2, 3) if k >= 25 or k % 4 != 2 else (3,)):
                nc.scalar.activation(out=zfs[k][:, t, :], in_=zps[(k, 1)][:, t - 2, :], func=ACT.Identity,
                                     bias=b32[:, t:t + 1], scale=1.0)

        def ev(k, h):
            zp = zps.pop((k, h))
            if h == 0 or k < 4:
                nc.vector.tensor_tensor(out=zfs[k][:, 2 * h:2 * h + 2, :], in0=zp[:],
                                        in1=b32[:, 2 * h:2 * h + 2].unsqueeze(2).to_broadcast([P, 2, 2 * P]), op=ALU.add)
            elif not (k >= 25 or k % 4 != 2):
                nc.vector.tensor_scalar(out=zfs[k][:, 2, :], in0=zp[:, 0, :], scalar1=b32[:, 2:3], scalar2=None,
                                        op0=ALU.add)

        def cast(k):
            zg = work.tile([P, 2, P, 4], BF16, tag="zg", bufs=1, align_bytes=64, name="zg")
            nc.gpsimd.tensor_scalar(out=zg[:].rearrange("p a (c i) t -> p (a c) t i", i=4),
                                    in0=zfs[k][:].rearrange("p t (c i) -> p c t i", i=4), scalar1=1.0, scalar2=0.0,
                                    op0=ALU.mult, op1=ALU.add)
            zgs[k] = zg

        def by_gram(k, a):
            return a == 1 and k % 2 == 0 and 4 <= k

        def diag(k, a):
            n = 2 * k + a
            gjunk = work.tile([P, P], BF16, tag="gjunk", bufs=4, name="gjunk")
            nc.vector.scalar_tensor_tensor(out=gjunk[:], in0=z2ps.pop((k, a))[:, 0, :], scalar=s_ap[:, 0:1], in1=identf[:],
                                           op0=ALU.mult, op1=ALU.mult, accum_out=a_all[:, n:n + 1])

        def sq(k, a):
            if by_gram(k, a):
                return
            n = 2 * k + a
            sjunk = work.tile([P, 4 * P], BF16, tag="sjunk", bufs=8, name="sjunk")
            nc.scalar.activation(out=sjunk[:], in_=z2ps.pop((k, a))[:].rearrange("p t c -> p (t c)"), func=ACT.Square,
                                 scale=rsq[:, 0:1], accum_out=a_all[:, n:n + 1])

        def q_z(k):
            zg = zgs.pop(k)
            zc = work.tile([P, 2 * P], U32, tag="zc", bufs=3, align_bytes=64, name="zc")
            zs = work.tile([P, 2 * P], U8, tag="zs", bufs=3, align_bytes=64, name="zs")
            nc.vector.quantize_mx(out=zc[:].bitcast(FP8X4), scales=zs[:], in_=zg[:].rearrange("p a i t -> p (a i t)"))
            zcodes[k] = (zc, zs)

        def s2(k):
            zc, zs = zcodes.pop(k)
            gp = psum.tile([P, 2, NREF], F32, tag="G", bufs=PS_BUFS["G"], name="gp")
            for a in range(2):
                nc.tensor.matmul_mx(out=gp[:, a, :],
                                    lhsT=zc[:, P * a:P * a + P].bitcast(FP8X4), lhsT_scale=zs[:, P * a:P * a + P],
                                    rhs=rc[:].bitcast(FP8X4), rhs_scale=rsc[:], start=True, stop=True)
            gps[k] = gp

        def z2(k):
            zf = zfs.pop(k)
            for a in range(2):
                ztp = psum.tile([P, 4, P], F32, tag="ZT", bufs=PS_BUFS["ZT"], name="ztp")
                for t in range(4):
                    zt = zf[:, t, P * a:P * a + P]
                    if by_gram(k, a):
                        nc.tensor.matmul(out=ztp[:, 0, :], lhsT=zt, rhs=zt, start=t == 0, stop=t == 3)
                    else:
                        nc.tensor.transpose(ztp[:, t, :], zt, identf[:])
                z2ps[(k, a)] = ztp

        def nega(k):
            nc.gpsimd.tensor_scalar(out=nega_all[:, 2 * k - 2:2 * k + 2], in0=a_all[:, 2 * k - 2:2 * k + 2],
                                    scalar1=-1.0, scalar2=0.0, op0=ALU.mult, op1=ALU.add)

        def stt(k):
            u = work.tile([P, 2, NREF], F32, tag="u", bufs=4, name="u")
            nc.vector.scalar_tensor_tensor(out=u[:], in0=gps.pop(k)[:], scalar=n2s[:, 0:1],
                                           in1=csb[:].unsqueeze(1).to_broadcast([P, 2, NREF]),
                                           op0=ALU.mult, op1=ALU.add)
            us[k] = u

        def cm(k, a):
            if a == 0:
                ucls[k] = work.tile([P, 2, NREF], F32, tag="ucl", bufs=6, name="ucl")
            n = 2 * k + a
            nc.vector.tensor_scalar(out=ucls[k][:, a, :], in0=us[k][:, a, :], scalar1=nega_all[:, n:n + 1], scalar2=None,
                                    op0=ALU.max, op1=ALU.min, accum_out=mn_all[:, n:n + 1])

        def ex(k, a):
            n = 2 * k + a
            ejunk = work.tile([P, NREF], BF16, tag="ejunk", bufs=8, name="ejunk")
            nc.scalar.activation(out=ejunk[:], in_=ucls[k][:, a, :], func=ACT.Exp, bias=mn_all[:, n:n + 1], scale=-1.0,
                                 accum_out=sum_all[:, n:n + 1])

        LN0 = 3
        SER0 = LN0 + len(ln_steps) - 3

        def x_steps(j):
            first = {1: 3, 2: 5}.get(j, j + 4)
            return [k for k in ([first, first + 1] if j < 3 else [first]) if k < NPAIR]

        def x_step(k):
            copy_out(k, on_vector=k == 3)
            if k + 1 < NPAIR and k + 1 != 4:
                t_x(k + 1)

        def cms(k):
            if valid(k):
                cm(k, 0)
                cm(k, 1)

        s1(0, 0)
        copy_out(1)
        t_x(2, "ZT")
        s1(0, 1)
        q_x(1)
        r_square(0)
        s1(1, 0)
        nc.vector.tensor_tensor(out=hh[:], in0=h32[:], in1=h32[:], op=ALU.mult)
        nc.vector.reciprocal(out=rinv[:], in_=h32[:])
        plane(0)
        ev(0, 0)
        copy_out(2)
        s1(1, 1)
        nc.vector.reciprocal(out=rh[:], in_=hh[:])
        nc.vector.tensor_scalar(out=rsq[:], in0=rinv[:], scalar1=math.sqrt(0.5), scalar2=None, op0=ALU.mult)
        ev(0, 1)
        t_x(3)
        q_x(2)
        cast(0)
        nc.vector.tensor_scalar(out=n2s[:], in0=rh[:], scalar1=-1.0, scalar2=None, op0=ALU.mult)
        nc.vector.tensor_scalar(out=s_ap[:], in0=rh[:], scalar1=0.5, scalar2=None, op0=ALU.mult)
        transposes("r", [r32[:, i // 2, (i % 2):256:2] for i in range(4)], "G")
        t_x(4, "G")
        r_square(1)
        copy_out("r")
        for j in range(1, NPAIR + 5):
            xs_now = x_steps(j)
            if valid(j + 1):
                s1(j + 1, 0)
            if valid(j - 1):
                z2(j - 1)
            if xs_now:
                x_step(xs_now[0])
            if j == 2:
                r2t = psum.tile([P, 2, P], F32, tag="G", bufs=PS_BUFS["G"], name="r2t")
                for jt in range(2):
                    nc.tensor.matmul(out=r2t[:, jt, :], lhsT=r2[:, jt:jt + 1].to_broadcast([P, P]), rhs=identf[:],
                                     start=True, stop=True)
            if valid(j):
                plane(j)
                ev(j, 0)
            if valid(j + 1):
                s1(j + 1, 1)
            for k in xs_now[1:]:
                x_step(k)
            if valid(j):
                ev(j, 1)
            if j < NPAIR:
                if valid(j - 3):
                    stt(j - 3)
                cms(j - 4)
            for a in range(2):
                if valid(j - 1) and by_gram(j - 1, a):
                    diag(j - 1, a)
            for k in xs_now:
                if j == 2 and k == xs_now[-1]:
                    for step in ln_steps[:4]:
                        step()
                q_x(k)
            if j == NPAIR:
                stt(j - 3)
                cms(j - 4)
                s2(j - 2)
                stt(j - 2)
            if valid(j - 1):
                q_z(j - 1)
            if j < NPAIR and valid(j - 2):
                s2(j - 2)
            if j == NPAIR + 1:
                s2(j - 2)
                cms(j - 4)
                stt(j - 2)
                cms(j - 3)
                cms(j - 2)
            if j == 1:
                quantise("r", rc[:], rsc[:])
            if LN0 <= j < LN0 + len(ln_steps) - 4:
                ln_steps[j - LN0 + 4]()
            if SER0 <= j < SER0 + len(series_steps):
                series_steps[j - SER0]()
            if valid(j - 2) and j % 2 == 1 and j < NPAIR:
                nega(j - 2)
            if valid(j):
                cast(j)
            if j == 2:
                nc.scalar.activation(out=csb[:], in_=r2t[:].rearrange("p a j -> p (a j)"), func=ACT.Copy,
                                     scale=s_ap[:, 0:1])
            if valid(j - 5):
                ex(j - 5, 0)
                ex(j - 5, 1)
            if valid(j - 1):
                sq(j - 1, 0)
                sq(j - 1, 1)
                if j == NPAIR:
                    nega(j - 1)

        base = const.tile([P, NT], F32)
        nc.vector.scalar_tensor_tensor(out=base[:], in0=nega_all[:], scalar=coeff[:, 0:1], in1=mn_all[:],
                                       op0=ALU.add, op1=ALU.subtract)
        lns = const.tile([P, NT], F32)
        nc.scalar.activation(out=lns[:], in_=sum_all[:], func=ACT.Ln)
        res = const.tile([P, NT], F32)
        nc.vector.tensor_tensor(out=res[:], in0=lns[:], in1=base[:], op=ALU.add)
        nc.sync.dma_start(out=out.rearrange("(p n) -> p n", n=NT), in_=res[:])
